import numpy as np
import ml_dtypes


def mxq(x, axis, fmt="e4m3"):
    dtype, down = {"e4m3": (ml_dtypes.float8_e4m3fn, 7), "e5m2": (ml_dtypes.float8_e5m2, 14)}[fmt]
    v = np.moveaxis(np.asarray(x, np.float32).astype(ml_dtypes.bfloat16).astype(np.float64), axis, -1)
    blocks = v.reshape(v.shape[:-1] + (-1, 32))
    amax = np.abs(blocks).max(-1, keepdims=True)
    byte = np.maximum(np.where(amax > 0, np.frexp(amax)[1] - 1 + 127, 0) - down, 1)
    scale = np.exp2(byte - 127.0)
    codes = (blocks / scale).astype(np.float32).astype(dtype).astype(np.float64)
    return np.moveaxis((codes * scale).reshape(v.shape), -1, axis)


WIDE = False


def mx_kscale(k):
    if not WIDE:
        return np.ones(k)
    levels = np.array([10, -10, 5, -5, 0])
    a = np.random.permutation(np.resize(levels, k // 512 * 4)).reshape(k // 512, 4)
    idx = np.arange(k)
    return np.exp2(a[idx // 512, idx % 128 // 32])


BF16 = ml_dtypes.bfloat16


def bf(x):
    return np.asarray(x, np.float32).astype(BF16)


def f64(x):
    return np.asarray(x).astype(np.float64)


B, S, D, H, HD = 8, 512, 512, 2, 128
E = H * HD
EPS = 1e-5
NEG = -1e9


def get_slopes(n):
    start = 2.0 ** (-2.0 ** (-(np.log2(n) - 3)))
    return np.array([start * start ** i for i in range(n)])


def prior_bias(shape, scale, loc):
    q_pos = np.arange(S, dtype=np.float64)
    k_pos = np.arange(S, dtype=np.float64)
    dist = (k_pos[None, :] - q_pos[:, None])[None, None]
    loc_t = np.exp(loc) - np.exp(-loc)
    z = (dist - loc_t) * np.exp(scale)
    return -(np.abs(z) + EPS) ** shape


def setup_inputs():
    s = mx_kscale(D)
    causal = np.tril(np.ones((S, S), dtype=bool))
    return {"x": bf(np.random.standard_normal((B, S, D)) * s),
            "wv": bf(np.random.standard_normal((D, E)) * 2.0 / np.sqrt(D) / s[:, None]),
            "q": bf(np.random.standard_normal((B, S, H, HD))),
            "k": bf(np.random.standard_normal((B, S, H, HD))),
            "mask": bf(np.where(causal, 0.0, NEG))[None, None],
            "shape": bf(1.0 + 0.1 * np.random.standard_normal((1, H, 1, 1))),
            "scale": bf(np.log(get_slopes(H)).reshape(1, H, 1, 1) + 0.1 * np.random.standard_normal((1, H, 1, 1))),
            "loc": bf(-2.0 + 0.5 * np.random.standard_normal((1, H, 1, 1)))}


def reference(x, wv, q, k, mask, shape, scale, loc):
    v = (mxq(f64(x), 2, "e4m3") @ mxq(f64(wv), 0, "e4m3")).reshape(B, S, H, HD)
    s = f64(q).transpose(0, 2, 1, 3) @ f64(k).transpose(0, 2, 3, 1) / np.sqrt(HD)
    s = s + prior_bias(f64(shape), f64(scale), f64(loc))
    s = s + f64(mask)
    e = np.exp(s - s.max(-1, keepdims=True))
    o = (mxq(e, 3, "e4m3") @ mxq(v.transpose(0, 2, 1, 3), 2, "e4m3")) / e.sum(-1, keepdims=True)
    return o.transpose(0, 2, 1, 3).reshape(B, S, E)

@@ -1,0 +1,312 @@
+import math
+from contextlib import ExitStack
+
+import concourse.mybir as mybir
+from concourse.masks import make_identity
+
+F32 = mybir.dt.float32
+BF16 = mybir.dt.bfloat16
+U32 = mybir.dt.uint32
+U8 = mybir.dt.uint8
+FP8X4 = mybir.dt.float8_e4m3fn_x4
+ACT = mybir.ActivationFunctionType
+ALU = mybir.AluOpType
+AXIS = mybir.AxisListType
+
+B, S, D, H, HD = 8, 512, 512, 2, 128
+E = H * HD
+EPS = 1e-5
+P = 128
+T = 4
+GROUPS = B * H
+OFFSETS = 2 * T - 1
+
+FLOPS = 2 * B * S * D * E + 2 * 2 * B * H * S * S * HD
+
+
+def tile_bayesianattention_pa_t_kernel(tc, x, wv, q, k, mask, shape, scale, loc, out):
+    nc = tc.nc
+    with ExitStack() as ctx:
+        const = ctx.enter_context(tc.tile_pool(name="const", bufs=1))
+        inputs = ctx.enter_context(tc.tile_pool(name="inputs", bufs=B))
+        batch = ctx.enter_context(tc.tile_pool(name="batch", bufs=2))
+        group = ctx.enter_context(tc.tile_pool(name="group", bufs=3))
+        psum_prep = ctx.enter_context(tc.psum_pool(name="psum_prep", bufs=2))
+        psum_s = ctx.enter_context(tc.psum_pool(name="psum_s", bufs=3))
+        psum_et = ctx.enter_context(tc.psum_pool(name="psum_et", bufs=2))
+        psum_o = ctx.enter_context(tc.psum_pool(name="psum_o", bufs=1))
+
+        def load_parameter(param, name):
+            row = const.tile([P, H], BF16, name=name)
+            nc.sync.dma_start(
+                out=row[:], in_=param.rearrange("a h b c -> (a h b c)").partition_broadcast(P)
+            )
+            return row
+
+        scale_bf = load_parameter(scale, "scale_bf")
+        loc_bf = load_parameter(loc, "loc_bf")
+        shape_bf = load_parameter(shape, "shape_bf")
+
+        q_in, k_in, x_in = {}, {}, {}
+
+        def load_batch(b):
+            q_sb = inputs.tile([P, T, E], BF16, tag="q")
+            nc.sync.dma_start(out=q_sb[:], in_=q[b].rearrange("(p t) h d -> p t (h d)", t=T))
+            k_sb = inputs.tile([P, T, E], BF16, tag="k")
+            nc.sync.dma_start(out=k_sb[:], in_=k[b].rearrange("(p t) h d -> p t (h d)", t=T))
+            x_sb = inputs.tile([P, T, D], BF16, tag="x")
+            nc.sync.dma_start(out=x_sb[:], in_=x[b].rearrange("(p t) f -> p t f", t=T))
+            q_in[b], k_in[b], x_in[b] = q_sb, k_sb, x_sb
+
+        mask_sb = const.tile([P, T, S], BF16)
+        nc.sync.dma_start(out=mask_sb[:], in_=mask[0, 0].rearrange("(p t) j -> p t j", t=T))
+        wv_sb = const.tile([P, T, E], BF16)
+        for u in range(2):
+            nc.sync.dma_start(
+                out=wv_sb[:, 2 * u : 2 * u + 2, :],
+                in_=wv[2 * P * u : 2 * P * (u + 1), :].rearrange("(p e) c -> p e c", e=2),
+            )
+        for b in range(B):
+            load_batch(b)
+
+        ident_bf = const.tile([P, P], BF16)
+        make_identity(nc, ident_bf[:])
+        ident_f32 = const.tile([P, P], F32)
+        make_identity(nc, ident_f32[:])
+
+        dist = const.tile([P, OFFSETS, P], F32)
+        nc.gpsimd.iota(
+            dist[:],
+            pattern=[[-1, OFFSETS], [-T, P]],
+            base=T - 1,
+            channel_multiplier=T,
+            allow_small_or_imprecise_dtypes=True,
+        )
+        slope = const.tile([P, H], F32)
+        nc.scalar.activation(out=slope[:], in_=scale_bf[:], func=ACT.Exp)
+        exp_loc = const.tile([P, H], F32)
+        nc.scalar.activation(out=exp_loc[:], in_=loc_bf[:], func=ACT.Exp)
+        exp_neg_loc = const.tile([P, H], F32)
+        nc.scalar.activation(out=exp_neg_loc[:], in_=loc_bf[:], func=ACT.Exp, scale=-1.0)
+        shift = const.tile([P, H], F32)
+        nc.vector.tensor_sub(out=shift[:], in0=exp_neg_loc[:], in1=exp_loc[:])
+        nc.vector.tensor_mul(out=shift[:], in0=shift[:], in1=slope[:])
+        power = const.tile([P, H], F32)
+        nc.vector.tensor_copy(out=power[:], in_=shape_bf[:])
+
+        prior = []
+        for h in range(H):
+            prior_h = const.tile([P, OFFSETS, P], F32, name="prior%d" % h)
+            prior.append(prior_h)
+            nc.scalar.activation(
+                out=prior_h[:], in_=dist[:], func=ACT.Abs,
+                scale=slope[:, h : h + 1], bias=shift[:, h : h + 1],
+            )
+        for h in range(H):
+            nc.scalar.activation(out=prior[h][:], in_=prior[h][:], func=ACT.Ln, bias=EPS)
+        for h in range(H):
+            nc.scalar.activation(
+                out=prior[h][:], in_=prior[h][:], func=ACT.Exp,
+                scale=power[:, h : h + 1], bias=0.5 * math.log(HD),
+            )
+
+        mask_rows = const.tile([P, T, T, P], BF16)
+        nc.vector.tensor_copy(out=mask_rows[:], in_=mask_sb[:].rearrange("p a (j t) -> p a t j", t=T))
+        mask_t = []
+        for half in range(2):
+            mask_ps = psum_prep.tile([P, 2, T, P], BF16, tag="prep")
+            mask_t.append(mask_ps)
+            for t2 in range(2):
+                for ti in range(T):
+                    nc.tensor.transpose(
+                        mask_ps[:, t2, ti, :], mask_rows[:, ti, 2 * half + t2, :], ident_bf[:]
+                    )
+        added = []
+        for h in range(H):
+            added_h = const.tile([P, T, T, P], F32, name="added%d" % h)
+            added.append(added_h)
+            for t in range(T):
+                nc.vector.scalar_tensor_tensor(
+                    out=added_h[:, t, :, :],
+                    in0=mask_t[t // 2][:, t % 2, :, :],
+                    scalar=math.sqrt(HD),
+                    in1=prior[h][:, T - 1 - t : 2 * T - 1 - t, :],
+                    op0=ALU.mult,
+                    op1=ALU.subtract,
+                )
+
+        wv_grouped = const.tile([P, E, T], BF16, align_bytes=64)
+        nc.vector.tensor_copy(out=wv_grouped[:], in_=wv_sb[:].rearrange("p t c -> p c t"))
+        wv_codes = const.tile([P, E], U32, align_bytes=64)
+        wv_scales = const.tile([P, E], U8, align_bytes=64)
+        nc.vector.quantize_mx(
+            out=wv_codes[:].bitcast(FP8X4),
+            scales=wv_scales[:],
+            in_=wv_grouped[:].rearrange("p c t -> p (c t)"),
+        )
+
+        q_t, k_t, x_codes, x_scales, v_codes, v_scales, o_out = {}, {}, {}, {}, {}, {}, {}
+
+        def transpose_inputs(b):
+            for src, dst, tag in ((q_in[b], q_t, "q_t"), (k_in[b], k_t, "k_t")):
+                t_ps = psum_prep.tile([P, H, T, P], BF16, tag="prep")
+                for h in range(H):
+                    for t in range(T):
+                        nc.tensor.transpose(
+                            t_ps[:, h, t, :], src[:, t, h * HD : (h + 1) * HD], ident_bf[:]
+                        )
+                t_sb = batch.tile([P, H, T, P], BF16, tag=tag)
+                nc.vector.tensor_copy(out=t_sb[:], in_=t_ps[:])
+                dst[b] = t_sb
+            x_grouped = batch.tile([P, T, P, T], BF16, tag="x_grouped", align_bytes=64)
+            for half in range(2):
+                x_ps = psum_prep.tile([P, 2, 2, P], F32, tag="prep")
+                for t2 in range(2):
+                    x_words = x_in[b][:, 2 * half + t2, :].bitcast(F32)
+                    for u in range(2):
+                        nc.tensor.transpose(
+                            x_ps[:, t2, u, :], x_words[:, u * P : (u + 1) * P], ident_f32[:]
+                        )
+                nc.vector.tensor_copy(
+                    out=x_grouped[:, 2 * half : 2 * half + 2, :, :].bitcast(F32),
+                    in_=x_ps[:].rearrange("p t u r -> p t r u"),
+                )
+            codes = batch.tile([P, T * P], U32, tag="x_codes", align_bytes=64)
+            scales = batch.tile([P, T * P], U8, tag="x_scales", align_bytes=64)
+            nc.vector.quantize_mx(
+                out=codes[:].bitcast(FP8X4),
+                scales=scales[:],
+                in_=x_grouped[:].rearrange("p t r w -> p (t r w)"),
+            )
+            x_codes[b], x_scales[b] = codes, scales
+
+        def project_values(b):
+            v_grouped = batch.tile([P, H, HD, T], BF16, tag="v_grouped", align_bytes=64)
+            for h in range(H):
+                v_ps = psum_prep.tile([P, T, HD], F32, tag="prep")
+                for t in range(T):
+                    nc.tensor.matmul_mx(
+                        out=v_ps[:, t, :],
+                        lhsT=x_codes[b][:, t * P : (t + 1) * P].bitcast(FP8X4),
+                        lhsT_scale=x_scales[b][:, t * P : (t + 1) * P],
+                        rhs=wv_codes[:, h * HD : (h + 1) * HD].bitcast(FP8X4),
+                        rhs_scale=wv_scales[:, h * HD : (h + 1) * HD],
+                        start=True,
+                        stop=True,
+                    )
+                nc.vector.tensor_copy(out=v_grouped[:, h, :, :], in_=v_ps[:].rearrange("p t d -> p d t"))
+            codes = batch.tile([P, E], U32, tag="v_codes", align_bytes=64)
+            scales = batch.tile([P, E], U8, tag="v_scales", align_bytes=64)
+            nc.vector.quantize_mx(
+                out=codes[:].bitcast(FP8X4),
+                scales=scales[:],
+                in_=v_grouped[:].rearrange("p h d t -> p (h d t)"),
+            )
+            v_codes[b], v_scales[b] = codes, scales
+
+        e_rows, row_sums, e_codes, e_scales = {}, {}, {}, {}
+
+        def scores_and_softmax(g):
+            b, h = divmod(g, H)
+            e_sb = group.tile([P, T, S], BF16, tag="e")
+            row_max = group.tile([P, T], F32, tag="row_max")
+            exp_bias = group.tile([P, T], F32, tag="exp_bias")
+            row_sum = group.tile([P, T], F32, tag="row_sum")
+            for ti in range(T):
+                s_ps = psum_s.tile([P, T, P], F32, tag="s")
+                nc.tensor.matmul(
+                    out=s_ps[:].rearrange("p t j -> p (t j)"),
+                    lhsT=q_t[b][:, h, ti, :],
+                    rhs=k_t[b][:, h, :, :].rearrange("p t j -> p (t j)"),
+                    start=True,
+                    stop=False,
+                )
+                for t in range(T):
+                    nc.tensor.matmul(
+                        out=s_ps[:, t, :],
+                        lhsT=added[h][:, t, ti, :],
+                        rhs=ident_f32[:],
+                        is_transpose=True,
+                        start=False,
+                        stop=(t == T - 1),
+                    )
+                nc.vector.reduce_max(
+                    out=row_max[:, ti : ti + 1], in_=s_ps[:].rearrange("p t j -> p (t j)"), axis=AXIS.X
+                )
+                nc.vector.tensor_scalar_mul(
+                    out=exp_bias[:, ti : ti + 1], in0=row_max[:, ti : ti + 1], scalar1=-1.0 / math.sqrt(HD)
+                )
+                nc.scalar.activation(
+                    out=e_sb[:, ti, :],
+                    in_=s_ps[:].rearrange("p t j -> p (t j)"),
+                    func=ACT.Exp,
+                    scale=1.0 / math.sqrt(HD),
+                    bias=exp_bias[:, ti : ti + 1],
+                    accum_out=row_sum[:, ti : ti + 1],
+                )
+            e_rows[g], row_sums[g] = e_sb, row_sum
+
+        def transpose_and_quantise(g):
+            e_grouped = group.tile([P, T, P, T], BF16, tag="e_grouped", align_bytes=64)
+            for half in range(2):
+                e_ps = psum_et.tile([P, 2, T, P], BF16, tag="et")
+                for t2 in range(2):
+                    for t in range(T):
+                        nc.tensor.transpose(
+                            e_ps[:, t2, t, :], e_rows[g][:, 2 * half + t2, t * P : (t + 1) * P], ident_bf[:]
+                        )
+                nc.scalar.copy(
+                    out=e_grouped[:, 2 * half : 2 * half + 2, :, :],
+                    in_=e_ps[:].rearrange("p a t i -> p a i t"),
+                )
+            codes = group.tile([P, T * P], U32, tag="e_codes", align_bytes=64)
+            scales = group.tile([P, T * P], U8, tag="e_scales", align_bytes=64)
+            nc.vector.quantize_mx(
+                out=codes[:].bitcast(FP8X4),
+                scales=scales[:],
+                in_=e_grouped[:].rearrange("p a i t -> p (a i t)"),
+            )
+            e_codes[g], e_scales[g] = codes, scales
+
+        def attend(g):
+            b, h = divmod(g, H)
+            if h == 0:
+                o_sb = batch.tile([P, T, E], F32, tag="o")
+                o_out[b] = o_sb
+            o_ps = psum_o.tile([P, T, HD], F32, tag="o_ps")
+            for ti in range(T):
+                nc.tensor.matmul_mx(
+                    out=o_ps[:, ti, :],
+                    lhsT=e_codes[g][:, ti * P : (ti + 1) * P].bitcast(FP8X4),
+                    lhsT_scale=e_scales[g][:, ti * P : (ti + 1) * P],
+                    rhs=v_codes[b][:, h * HD : (h + 1) * HD].bitcast(FP8X4),
+                    rhs_scale=v_scales[b][:, h * HD : (h + 1) * HD],
+                    start=True,
+                    stop=True,
+                )
+            inv_sum = group.tile([P, T], F32, tag="inv_sum")
+            nc.vector.reciprocal(out=inv_sum[:], in_=row_sums[g][:])
+            for ti in range(T):
+                nc.scalar.activation(
+                    out=o_out[b][:, ti, h * HD : (h + 1) * HD],
+                    in_=o_ps[:, ti, :],
+                    func=ACT.Copy,
+                    scale=inv_sum[:, ti : ti + 1],
+                )
+            if h == H - 1:
+                nc.sync.dma_start(out=out[b].rearrange("(p t) c -> p t c", t=T), in_=o_out[b][:])
+
+        transpose_inputs(0)
+        project_values(0)
+        for step in range(GROUPS + 2):
+            if step < GROUPS:
+                b, h = divmod(step, H)
+                if b + 1 < B and h == 0:
+                    transpose_inputs(b + 1)
+                if b + 1 < B and h == 1:
+                    project_values(b + 1)
+                scores_and_softmax(step)
+            if 1 <= step <= GROUPS:
+                transpose_and_quantise(step - 1)
+            if step >= 2:
+                attend(step - 2)

@@ -18,7 +18,8 @@ E = H * HD
 EPS = 1e-5
 P = 128
 T = 4
-GROUPS = B * H
+TILES = B * H * T
+TILES_PER_BATCH = H * T
 OFFSETS = 2 * T - 1
 
 FLOPS = 2 * B * S * D * E + 2 * 2 * B * H * S * S * HD
@@ -27,10 +28,12 @@ FLOPS = 2 * B * S * D * E + 2 * 2 * B * H * S * S * HD
 def tile_bayesianattention_pa_t_kernel(tc, x, wv, q, k, mask, shape, scale, loc, out):
     nc = tc.nc
     with ExitStack() as ctx:
+        ctx.enter_context(tc.manual_schedule())
         const = ctx.enter_context(tc.tile_pool(name="const", bufs=1))
         inputs = ctx.enter_context(tc.tile_pool(name="inputs", bufs=B))
         batch = ctx.enter_context(tc.tile_pool(name="batch", bufs=2))
-        group = ctx.enter_context(tc.tile_pool(name="group", bufs=3))
+        group = ctx.enter_context(tc.tile_pool(name="group", bufs=4))
+        rows = ctx.enter_context(tc.tile_pool(name="rows", bufs=3))
         psum_prep = ctx.enter_context(tc.psum_pool(name="psum_prep", bufs=2))
         psum_s = ctx.enter_context(tc.psum_pool(name="psum_s", bufs=3))
         psum_et = ctx.enter_context(tc.psum_pool(name="psum_et", bufs=2))
@@ -49,39 +52,54 @@ def tile_bayesianattention_pa_t_kernel(tc, x, wv, q, k, mask, shape, scale, loc,
 
         q_in, k_in, x_in = {}, {}, {}
 
-        def load_batch(b):
+        def load_queries_and_keys(b):
             q_sb = inputs.tile([P, T, E], BF16, tag="q")
             nc.sync.dma_start(out=q_sb[:], in_=q[b].rearrange("(p t) h d -> p t (h d)", t=T))
             k_sb = inputs.tile([P, T, E], BF16, tag="k")
             nc.sync.dma_start(out=k_sb[:], in_=k[b].rearrange("(p t) h d -> p t (h d)", t=T))
+            q_in[b], k_in[b] = q_sb, k_sb
+
+        def load_x(b):
             x_sb = inputs.tile([P, T, D], BF16, tag="x")
             nc.sync.dma_start(out=x_sb[:], in_=x[b].rearrange("(p t) f -> p t f", t=T))
-            q_in[b], k_in[b], x_in[b] = q_sb, k_sb, x_sb
+            x_in[b] = x_sb
 
-        mask_sb = const.tile([P, T, S], BF16)
-        nc.sync.dma_start(out=mask_sb[:], in_=mask[0, 0].rearrange("(p t) j -> p t j", t=T))
+        load_queries_and_keys(0)
         wv_sb = const.tile([P, T, E], BF16)
         for u in range(2):
             nc.sync.dma_start(
                 out=wv_sb[:, 2 * u : 2 * u + 2, :],
                 in_=wv[2 * P * u : 2 * P * (u + 1), :].rearrange("(p e) c -> p e c", e=2),
             )
-        for b in range(B):
-            load_batch(b)
+        load_x(0)
+        mask_sb = const.tile([P, T, S], BF16)
+        nc.sync.dma_start(out=mask_sb[:], in_=mask[0, 0].rearrange("(p t) j -> p t j", t=T))
+        for b in range(1, B):
+            load_queries_and_keys(b)
+            load_x(b)
 
         ident_bf = const.tile([P, P], BF16)
         make_identity(nc, ident_bf[:])
-        ident_f32 = const.tile([P, P], F32)
-        make_identity(nc, ident_f32[:])
-
-        dist = const.tile([P, OFFSETS, P], F32)
+        dist_partitions = const.tile([P, P], F32)
         nc.gpsimd.iota(
-            dist[:],
-            pattern=[[-1, OFFSETS], [-T, P]],
-            base=T - 1,
-            channel_multiplier=T,
+            dist_partitions[:], pattern=[[-T, P]], base=0, channel_multiplier=T,
             allow_small_or_imprecise_dtypes=True,
         )
+        dist_rows = const.tile([P, OFFSETS], F32)
+        nc.gpsimd.iota(
+            dist_rows[:], pattern=[[1, OFFSETS]], base=1 - T, channel_multiplier=0,
+            allow_small_or_imprecise_dtypes=True,
+        )
+        ident_f32 = const.tile([P, P], F32)
+        make_identity(nc, ident_f32[:])
+        dist = const.tile([P, OFFSETS, P], F32)
+        nc.vector.tensor_tensor(
+            out=dist[:],
+            in0=dist_partitions[:].unsqueeze(1).to_broadcast([P, OFFSETS, P]),
+            in1=dist_rows[:].unsqueeze(2).to_broadcast([P, OFFSETS, P]),
+            op=ALU.add,
+        )
+
         slope = const.tile([P, H], F32)
         nc.scalar.activation(out=slope[:], in_=scale_bf[:], func=ACT.Exp)
         exp_loc = const.tile([P, H], F32)
@@ -93,7 +111,6 @@ def tile_bayesianattention_pa_t_kernel(tc, x, wv, q, k, mask, shape, scale, loc,
         nc.vector.tensor_mul(out=shift[:], in0=shift[:], in1=slope[:])
         power = const.tile([P, H], F32)
         nc.vector.tensor_copy(out=power[:], in_=shape_bf[:])
-
         prior = []
         for h in range(H):
             prior_h = const.tile([P, OFFSETS, P], F32, name="prior%d" % h)
@@ -110,33 +127,91 @@ def tile_bayesianattention_pa_t_kernel(tc, x, wv, q, k, mask, shape, scale, loc,
                 scale=power[:, h : h + 1], bias=0.5 * math.log(HD),
             )
 
-        mask_rows = const.tile([P, T, T, P], BF16)
-        nc.vector.tensor_copy(out=mask_rows[:], in_=mask_sb[:].rearrange("p a (j t) -> p a t j", t=T))
-        mask_t = []
-        for half in range(2):
-            mask_ps = psum_prep.tile([P, 2, T, P], BF16, tag="prep")
-            mask_t.append(mask_ps)
-            for t2 in range(2):
-                for ti in range(T):
-                    nc.tensor.transpose(
-                        mask_ps[:, t2, ti, :], mask_rows[:, ti, 2 * half + t2, :], ident_bf[:]
-                    )
-        added = []
-        for h in range(H):
-            added_h = const.tile([P, T, T, P], F32, name="added%d" % h)
-            added.append(added_h)
-            for t in range(T):
-                nc.vector.scalar_tensor_tensor(
-                    out=added_h[:, t, :, :],
-                    in0=mask_t[t // 2][:, t % 2, :, :],
-                    scalar=math.sqrt(HD),
-                    in1=prior[h][:, T - 1 - t : 2 * T - 1 - t, :],
-                    op0=ALU.mult,
-                    op1=ALU.subtract,
-                )
+        waiting = {}
+        q_t, k_t, x_grouped, x_codes, x_scales = {}, {}, {}, {}, {}
+        v_grouped, v_codes, v_scales = {}, {}, {}
 
+        def transpose_heads(src):
+            t_ps = psum_prep.tile([P, H, T, P], BF16, tag="prep")
+            for h in range(H):
+                for t in range(T):
+                    nc.tensor.transpose(t_ps[:, h, t, :], src[:, t, h * HD : (h + 1) * HD], ident_bf[:])
+            return t_ps
+
+        def copy_heads(t_ps, tag, on_scalar):
+            t_sb = batch.tile([P, H, T, P], BF16, tag=tag)
+            if on_scalar:
+                nc.scalar.copy(out=t_sb[:], in_=t_ps[:])
+            else:
+                nc.vector.tensor_copy(out=t_sb[:], in_=t_ps[:])
+            return t_sb
+
+        def transpose_x(b, half):
+            x_ps = psum_prep.tile([P, 2, 2, P], F32, tag="prep")
+            for t2 in range(2):
+                x_words = x_in[b][:, 2 * half + t2, :].bitcast(F32)
+                for u in range(2):
+                    nc.tensor.transpose(x_ps[:, t2, u, :], x_words[:, u * P : (u + 1) * P], ident_f32[:])
+            return x_ps
+
+        def copy_x(b, half, x_ps):
+            if half == 0:
+                grouped = batch.tile([P, T, P, T], BF16, tag="x_grouped", align_bytes=64)
+                x_grouped[b] = grouped
+            nc.vector.tensor_copy(
+                out=x_grouped[b][:, 2 * half : 2 * half + 2, :, :].bitcast(F32),
+                in_=x_ps[:].rearrange("p t u r -> p t r u"),
+            )
+
+        def quantise_x(b):
+            codes = batch.tile([P, T * P], U32, tag="x_codes", align_bytes=64)
+            scales = batch.tile([P, T * P], U8, tag="x_scales", align_bytes=64)
+            nc.vector.quantize_mx(
+                out=codes[:].bitcast(FP8X4),
+                scales=scales[:],
+                in_=x_grouped[b][:].rearrange("p t r w -> p (t r w)"),
+            )
+            x_codes[b], x_scales[b] = codes, scales
+
+        def project_values(b, h):
+            v_ps = psum_prep.tile([P, T, HD], F32, tag="prep")
+            for t in range(T):
+                nc.tensor.matmul_mx(
+                    out=v_ps[:, t, :],
+                    lhsT=x_codes[b][:, t * P : (t + 1) * P].bitcast(FP8X4),
+                    lhsT_scale=x_scales[b][:, t * P : (t + 1) * P],
+                    rhs=wv_codes[:, h * HD : (h + 1) * HD].bitcast(FP8X4),
+                    rhs_scale=wv_scales[:, h * HD : (h + 1) * HD],
+                    start=True,
+                    stop=True,
+                )
+            return v_ps
+
+        def copy_values(b, h, v_ps):
+            if h == 0:
+                grouped = batch.tile([P, H, HD, T], BF16, tag="v_grouped", align_bytes=64)
+                v_grouped[b] = grouped
+            nc.vector.tensor_copy(out=v_grouped[b][:, h, :, :], in_=v_ps[:].rearrange("p t d -> p d t"))
+
+        def quantise_values(b):
+            codes = batch.tile([P, E], U32, tag="v_codes", align_bytes=64)
+            scales = batch.tile([P, E], U8, tag="v_scales", align_bytes=64)
+            nc.vector.quantize_mx(
+                out=codes[:].bitcast(FP8X4),
+                scales=scales[:],
+                in_=v_grouped[b][:].rearrange("p h d t -> p (h d t)"),
+            )
+            v_codes[b], v_scales[b] = codes, scales
+
+        q_ps = transpose_heads(q_in[0])
+        k_ps = transpose_heads(k_in[0])
+        q_t[0] = copy_heads(q_ps, "q_t", False)
+        k_t[0] = copy_heads(k_ps, "k_t", False)
         wv_grouped = const.tile([P, E, T], BF16, align_bytes=64)
         nc.vector.tensor_copy(out=wv_grouped[:], in_=wv_sb[:].rearrange("p t c -> p c t"))
+        x_low = transpose_x(0, 0)
+        x_high = transpose_x(0, 1)
+        copy_x(0, 0, x_low)
         wv_codes = const.tile([P, E], U32, align_bytes=64)
         wv_scales = const.tile([P, E], U8, align_bytes=64)
         nc.vector.quantize_mx(
@@ -144,135 +219,122 @@ def tile_bayesianattention_pa_t_kernel(tc, x, wv, q, k, mask, shape, scale, loc,
             scales=wv_scales[:],
             in_=wv_grouped[:].rearrange("p c t -> p (c t)"),
         )
-
-        q_t, k_t, x_codes, x_scales, v_codes, v_scales, o_out = {}, {}, {}, {}, {}, {}, {}
-
-        def transpose_inputs(b):
-            for src, dst, tag in ((q_in[b], q_t, "q_t"), (k_in[b], k_t, "k_t")):
-                t_ps = psum_prep.tile([P, H, T, P], BF16, tag="prep")
-                for h in range(H):
-                    for t in range(T):
-                        nc.tensor.transpose(
-                            t_ps[:, h, t, :], src[:, t, h * HD : (h + 1) * HD], ident_bf[:]
-                        )
-                t_sb = batch.tile([P, H, T, P], BF16, tag=tag)
-                nc.vector.tensor_copy(out=t_sb[:], in_=t_ps[:])
-                dst[b] = t_sb
-            x_grouped = batch.tile([P, T, P, T], BF16, tag="x_grouped", align_bytes=64)
-            for half in range(2):
-                x_ps = psum_prep.tile([P, 2, 2, P], F32, tag="prep")
-                for t2 in range(2):
-                    x_words = x_in[b][:, 2 * half + t2, :].bitcast(F32)
-                    for u in range(2):
-                        nc.tensor.transpose(
-                            x_ps[:, t2, u, :], x_words[:, u * P : (u + 1) * P], ident_f32[:]
-                        )
-                nc.vector.tensor_copy(
-                    out=x_grouped[:, 2 * half : 2 * half + 2, :, :].bitcast(F32),
-                    in_=x_ps[:].rearrange("p t u r -> p t r u"),
-                )
-            codes = batch.tile([P, T * P], U32, tag="x_codes", align_bytes=64)
-            scales = batch.tile([P, T * P], U8, tag="x_scales", align_bytes=64)
-            nc.vector.quantize_mx(
-                out=codes[:].bitcast(FP8X4),
-                scales=scales[:],
-                in_=x_grouped[:].rearrange("p t r w -> p (t r w)"),
-            )
-            x_codes[b], x_scales[b] = codes, scales
-
-        def project_values(b):
-            v_grouped = batch.tile([P, H, HD, T], BF16, tag="v_grouped", align_bytes=64)
-            for h in range(H):
-                v_ps = psum_prep.tile([P, T, HD], F32, tag="prep")
+        copy_x(0, 1, x_high)
+        mask_rows = const.tile([P, T, T, P], BF16)
+        nc.vector.tensor_copy(out=mask_rows[:], in_=mask_sb[:].rearrange("p a (j t) -> p a t j", t=T))
+        quantise_x(0)
+        mask_t = const.tile([P, T, T, P], BF16)
+        mask_banks = []
+        for half in range(2):
+            mask_ps = psum_prep.tile([P, 2, T, P], BF16, tag="prep")
+            mask_banks.append(mask_ps)
+            for ti2 in range(2):
                 for t in range(T):
-                    nc.tensor.matmul_mx(
-                        out=v_ps[:, t, :],
-                        lhsT=x_codes[b][:, t * P : (t + 1) * P].bitcast(FP8X4),
-                        lhsT_scale=x_scales[b][:, t * P : (t + 1) * P],
-                        rhs=wv_codes[:, h * HD : (h + 1) * HD].bitcast(FP8X4),
-                        rhs_scale=wv_scales[:, h * HD : (h + 1) * HD],
-                        start=True,
-                        stop=True,
+                    nc.tensor.transpose(
+                        mask_ps[:, ti2, t, :], mask_rows[:, 2 * half + ti2, t, :], ident_bf[:]
                     )
-                nc.vector.tensor_copy(out=v_grouped[:, h, :, :], in_=v_ps[:].rearrange("p t d -> p d t"))
-            codes = batch.tile([P, E], U32, tag="v_codes", align_bytes=64)
-            scales = batch.tile([P, E], U8, tag="v_scales", align_bytes=64)
-            nc.vector.quantize_mx(
-                out=codes[:].bitcast(FP8X4),
-                scales=scales[:],
-                in_=v_grouped[:].rearrange("p h d t -> p (h d t)"),
+        for half in range(2):
+            nc.vector.tensor_copy(out=mask_t[:, 2 * half : 2 * half + 2, :, :], in_=mask_banks[half][:])
+        v_low = project_values(0, 0)
+        v_high = project_values(0, 1)
+        copy_values(0, 0, v_low)
+        copy_values(0, 1, v_high)
+        quantise_values(0)
+
+        added = []
+        for h in range(H):
+            added_h = const.tile([P, T, T, P], F32, name="added%d" % h)
+            added.append(added_h)
+        s_banks, e_rows, e_banks, e_groups = {}, {}, {}, {}
+        row_max, exp_bias, row_sum, e_codes, e_scales, o_banks = {}, {}, {}, {}, {}, {}
+
+        def add_prior_and_mask(n):
+            h, ti = divmod(n, T)
+            nc.vector.scalar_tensor_tensor(
+                out=added[h][:, ti, :, :],
+                in0=mask_t[:, ti, :, :],
+                scalar=math.sqrt(HD),
+                in1=prior[h][:, T - 1 - ti : 2 * T - 1 - ti, :],
+                op0=ALU.mult,
+                op1=ALU.subtract,
             )
-            v_codes[b], v_scales[b] = codes, scales
 
-        e_rows, row_sums, e_codes, e_scales = {}, {}, {}, {}
-
-        def scores_and_softmax(g):
+        def scores(n):
+            g, ti = divmod(n, T)
             b, h = divmod(g, H)
-            e_sb = group.tile([P, T, S], BF16, tag="e")
-            row_max = group.tile([P, T], F32, tag="row_max")
-            exp_bias = group.tile([P, T], F32, tag="exp_bias")
-            row_sum = group.tile([P, T], F32, tag="row_sum")
-            for ti in range(T):
-                s_ps = psum_s.tile([P, T, P], F32, tag="s")
-                nc.tensor.matmul(
-                    out=s_ps[:].rearrange("p t j -> p (t j)"),
-                    lhsT=q_t[b][:, h, ti, :],
-                    rhs=k_t[b][:, h, :, :].rearrange("p t j -> p (t j)"),
-                    start=True,
-                    stop=False,
-                )
-                for t in range(T):
-                    nc.tensor.matmul(
-                        out=s_ps[:, t, :],
-                        lhsT=added[h][:, t, ti, :],
-                        rhs=ident_f32[:],
-                        is_transpose=True,
-                        start=False,
-                        stop=(t == T - 1),
-                    )
-                nc.vector.reduce_max(
-                    out=row_max[:, ti : ti + 1], in_=s_ps[:].rearrange("p t j -> p (t j)"), axis=AXIS.X
-                )
-                nc.vector.tensor_scalar_mul(
-                    out=exp_bias[:, ti : ti + 1], in0=row_max[:, ti : ti + 1], scalar1=-1.0 / math.sqrt(HD)
-                )
-                nc.scalar.activation(
-                    out=e_sb[:, ti, :],
-                    in_=s_ps[:].rearrange("p t j -> p (t j)"),
-                    func=ACT.Exp,
-                    scale=1.0 / math.sqrt(HD),
-                    bias=exp_bias[:, ti : ti + 1],
-                    accum_out=row_sum[:, ti : ti + 1],
-                )
-            e_rows[g], row_sums[g] = e_sb, row_sum
-
-        def transpose_and_quantise(g):
-            e_grouped = group.tile([P, T, P, T], BF16, tag="e_grouped", align_bytes=64)
-            for half in range(2):
-                e_ps = psum_et.tile([P, 2, T, P], BF16, tag="et")
-                for t2 in range(2):
-                    for t in range(T):
-                        nc.tensor.transpose(
-                            e_ps[:, t2, t, :], e_rows[g][:, 2 * half + t2, t * P : (t + 1) * P], ident_bf[:]
-                        )
-                nc.scalar.copy(
-                    out=e_grouped[:, 2 * half : 2 * half + 2, :, :],
-                    in_=e_ps[:].rearrange("p a t i -> p a i t"),
-                )
-            codes = group.tile([P, T * P], U32, tag="e_codes", align_bytes=64)
-            scales = group.tile([P, T * P], U8, tag="e_scales", align_bytes=64)
-            nc.vector.quantize_mx(
-                out=codes[:].bitcast(FP8X4),
-                scales=scales[:],
-                in_=e_grouped[:].rearrange("p a i t -> p (a i t)"),
+            s_ps = psum_s.tile([P, T, P], F32, tag="s")
+            nc.tensor.matmul(
+                out=s_ps[:].rearrange("p t j -> p (t j)"),
+                lhsT=q_t[b][:, h, ti, :],
+                rhs=k_t[b][:, h, :, :].rearrange("p t j -> p (t j)"),
+                start=True,
+                stop=False,
             )
-            e_codes[g], e_scales[g] = codes, scales
+            for t in range(T):
+                nc.tensor.matmul(
+                    out=s_ps[:, t, :],
+                    lhsT=added[h][:, ti, t, :],
+                    rhs=ident_f32[:],
+                    is_transpose=True,
+                    start=False,
+                    stop=(t == T - 1),
+                )
+            s_banks[n] = s_ps
+
+        def row_maximum(n):
+            g, ti = divmod(n, T)
+            if ti == 0:
+                maxima = group.tile([P, T], F32, tag="row_max")
+                biases = group.tile([P, T], F32, tag="exp_bias")
+                row_max[g], exp_bias[g] = maxima, biases
+            nc.vector.reduce_max(
+                out=row_max[g][:, ti : ti + 1], in_=s_banks[n][:].rearrange("p t j -> p (t j)"), axis=AXIS.X
+            )
+            nc.vector.tensor_scalar_mul(
+                out=exp_bias[g][:, ti : ti + 1], in0=row_max[g][:, ti : ti + 1], scalar1=-1.0 / math.sqrt(HD)
+            )
+
+        def exponent(n):
+            g, ti = divmod(n, T)
+            if ti == 0:
+                sums = group.tile([P, T], F32, tag="row_sum")
+                row_sum[g] = sums
+            e_sb = rows.tile([P, T, P], BF16, tag="e")
+            nc.scalar.activation(
+                out=e_sb[:].rearrange("p t j -> p (t j)"),
+                in_=s_banks[n][:].rearrange("p t j -> p (t j)"),
+                func=ACT.Exp,
+                scale=1.0 / math.sqrt(HD),
+                bias=exp_bias[g][:, ti : ti + 1],
+                accum_out=row_sum[g][:, ti : ti + 1],
+            )
+            e_rows[n] = e_sb
+
+        def transpose_e(n):
+            e_ps = psum_et.tile([P, T, P], BF16, tag="et")
+            for t in range(T):
+                nc.tensor.transpose(e_ps[:, t, :], e_rows[n][:, t, :], ident_bf[:])
+            e_banks[n] = e_ps
+
+        def group_e(n):
+            e_grouped = rows.tile([P, P, T], BF16, tag="e_grouped", align_bytes=64)
+            nc.scalar.copy(out=e_grouped[:], in_=e_banks[n][:].rearrange("p t i -> p i t"))
+            e_groups[n] = e_grouped
+
+        def quantise_e(n):
+            g, ti = divmod(n, T)
+            if ti == 0:
+                codes = group.tile([P, T * P], U32, tag="e_codes", align_bytes=64)
+                scales = group.tile([P, T * P], U8, tag="e_scales", align_bytes=64)
+                e_codes[g], e_scales[g] = codes, scales
+            nc.vector.quantize_mx(
+                out=e_codes[g][:, ti * P : (ti + 1) * P].bitcast(FP8X4),
+                scales=e_scales[g][:, ti * P : (ti + 1) * P],
+                in_=e_groups[n][:].rearrange("p i t -> p (i t)"),
+            )
 
         def attend(g):
             b, h = divmod(g, H)
-            if h == 0:
-                o_sb = batch.tile([P, T, E], F32, tag="o")
-                o_out[b] = o_sb
             o_ps = psum_o.tile([P, T, HD], F32, tag="o_ps")
             for ti in range(T):
                 nc.tensor.matmul_mx(
@@ -284,29 +346,76 @@ def tile_bayesianattention_pa_t_kernel(tc, x, wv, q, k, mask, shape, scale, loc,
                     start=True,
                     stop=True,
                 )
-            inv_sum = group.tile([P, T], F32, tag="inv_sum")
-            nc.vector.reciprocal(out=inv_sum[:], in_=row_sums[g][:])
-            for ti in range(T):
-                nc.scalar.activation(
-                    out=o_out[b][:, ti, h * HD : (h + 1) * HD],
-                    in_=o_ps[:, ti, :],
-                    func=ACT.Copy,
-                    scale=inv_sum[:, ti : ti + 1],
-                )
-            if h == H - 1:
-                nc.sync.dma_start(out=out[b].rearrange("(p t) c -> p t c", t=T), in_=o_out[b][:])
+            o_banks[g] = o_ps
 
-        transpose_inputs(0)
-        project_values(0)
-        for step in range(GROUPS + 2):
-            if step < GROUPS:
-                b, h = divmod(step, H)
-                if b + 1 < B and h == 0:
-                    transpose_inputs(b + 1)
-                if b + 1 < B and h == 1:
-                    project_values(b + 1)
-                scores_and_softmax(step)
-            if 1 <= step <= GROUPS:
-                transpose_and_quantise(step - 1)
-            if step >= 2:
-                attend(step - 2)
+        def divide_and_store(g):
+            b, h = divmod(g, H)
+            inv_sum = group.tile([P, T], F32, tag="inv_sum")
+            nc.vector.reciprocal(out=inv_sum[:], in_=row_sum[g][:])
+            o_sb = group.tile([P, T, HD], F32, tag="o")
+            nc.vector.tensor_tensor(
+                out=o_sb[:],
+                in0=o_banks[g][:],
+                in1=inv_sum[:].unsqueeze(2).to_broadcast([P, T, HD]),
+                op=ALU.mult,
+            )
+            nc.sync.dma_start(
+                out=out[b].rearrange("(p t) c -> p t c", t=T)[:, :, h * HD : (h + 1) * HD], in_=o_sb[:]
+            )
+
+        def step(n):
+            if 0 <= n + 3 < TILES_PER_BATCH:
+                add_prior_and_mask(n + 3)
+            if 0 <= n - 1 < TILES:
+                transpose_e(n - 1)
+            if 0 <= n + 2 < TILES:
+                scores(n + 2)
+            if 0 <= n - 7 < TILES and (n - 7) % T == T - 1:
+                attend((n - 7) // T)
+            if 0 <= n + 1 < TILES:
+                row_maximum(n + 1)
+            if 0 <= n < TILES:
+                exponent(n)
+            if 0 <= n - 2 < TILES:
+                group_e(n - 2)
+            if 0 <= n - 3 < TILES:
+                quantise_e(n - 3)
+            if 0 <= n - 8 < TILES and (n - 8) % T == T - 1:
+                divide_and_store((n - 8) // T)
+
+        for b in range(-1, B + 1):
+            first = b * TILES_PER_BATCH
+            finish = 1 <= b < B
+            prepare = 0 <= b < B - 1
+            step(first)
+            if finish:
+                copy_values(b, 1, waiting["v1"])
+            if prepare:
+                waiting["q"] = transpose_heads(q_in[b + 1])
+            step(first + 1)
+            if finish:
+                quantise_values(b)
+            if prepare:
+                q_t[b + 1] = copy_heads(waiting["q"], "q_t", True)
+                waiting["k"] = transpose_heads(k_in[b + 1])
+            step(first + 2)
+            if prepare:
+                k_t[b + 1] = copy_heads(waiting["k"], "k_t", True)
+                waiting["x0"] = transpose_x(b + 1, 0)
+            step(first + 3)
+            if prepare:
+                copy_x(b + 1, 0, waiting["x0"])
+                waiting["x1"] = transpose_x(b + 1, 1)
+            step(first + 4)
+            if prepare:
+                copy_x(b + 1, 1, waiting["x1"])
+            step(first + 5)
+            if prepare:
+                quantise_x(b + 1)
+            step(first + 6)
+            if prepare:
+                waiting["v0"] = project_values(b + 1, 0)
+                waiting["v1"] = project_values(b + 1, 1)
+            step(first + 7)
+            if prepare:
+                copy_values(b + 1, 0, waiting["v0"])

@@ -235,18 +235,13 @@ def tile_bayesianattention_pa_t_kernel(tc, x, wv, q, k, mask, shape, scale, loc,
                     )
         for half in range(2):
             nc.vector.tensor_copy(out=mask_t[:, 2 * half : 2 * half + 2, :, :], in_=mask_banks[half][:])
-        v_low = project_values(0, 0)
-        v_high = project_values(0, 1)
-        copy_values(0, 0, v_low)
-        copy_values(0, 1, v_high)
-        quantise_values(0)
 
         added = []
         for h in range(H):
             added_h = const.tile([P, T, T, P], F32, name="added%d" % h)
             added.append(added_h)
         s_banks, e_rows, e_banks, e_groups = {}, {}, {}, {}
-        row_max, exp_bias, row_sum, e_codes, e_scales, o_banks = {}, {}, {}, {}, {}, {}
+        row_max, exp_bias, row_sum, inv_sum, e_codes, e_scales, o_banks = {}, {}, {}, {}, {}, {}, {}
 
         def add_prior_and_mask(n):
             h, ti = divmod(n, T)
@@ -290,6 +285,9 @@ def tile_bayesianattention_pa_t_kernel(tc, x, wv, q, k, mask, shape, scale, loc,
             nc.vector.reduce_max(
                 out=row_max[g][:, ti : ti + 1], in_=s_banks[n][:].rearrange("p t j -> p (t j)"), axis=AXIS.X
             )
+
+        def scale_maximum(n):
+            g, ti = divmod(n, T)
             nc.vector.tensor_scalar_mul(
                 out=exp_bias[g][:, ti : ti + 1], in0=row_max[g][:, ti : ti + 1], scalar1=-1.0 / math.sqrt(HD)
             )
@@ -348,74 +346,95 @@ def tile_bayesianattention_pa_t_kernel(tc, x, wv, q, k, mask, shape, scale, loc,
                 )
             o_banks[g] = o_ps
 
+        def invert_row_sums(g):
+            inverse = group.tile([P, T], F32, tag="inv_sum")
+            nc.vector.reciprocal(out=inverse[:], in_=row_sum[g][:])
+            inv_sum[g] = inverse
+
         def divide_and_store(g):
             b, h = divmod(g, H)
-            inv_sum = group.tile([P, T], F32, tag="inv_sum")
-            nc.vector.reciprocal(out=inv_sum[:], in_=row_sum[g][:])
             o_sb = group.tile([P, T, HD], F32, tag="o")
             nc.vector.tensor_tensor(
                 out=o_sb[:],
                 in0=o_banks[g][:],
-                in1=inv_sum[:].unsqueeze(2).to_broadcast([P, T, HD]),
+                in1=inv_sum[g][:].unsqueeze(2).to_broadcast([P, T, HD]),
                 op=ALU.mult,
             )
             nc.sync.dma_start(
                 out=out[b].rearrange("(p t) c -> p t c", t=T)[:, :, h * HD : (h + 1) * HD], in_=o_sb[:]
             )
 
-        def step(n):
+        def last_tile_of_group(n):
+            return 0 <= n < TILES and n % T == T - 1
+
+        def step_begin(n):
+            if 0 <= n + 1 < TILES:
+                row_maximum(n + 1)
             if 0 <= n + 3 < TILES_PER_BATCH:
                 add_prior_and_mask(n + 3)
             if 0 <= n - 1 < TILES:
                 transpose_e(n - 1)
             if 0 <= n + 2 < TILES:
                 scores(n + 2)
-            if 0 <= n - 7 < TILES and (n - 7) % T == T - 1:
+            if last_tile_of_group(n - 7):
                 attend((n - 7) // T)
-            if 0 <= n + 1 < TILES:
-                row_maximum(n + 1)
-            if 0 <= n < TILES:
-                exponent(n)
-            if 0 <= n - 2 < TILES:
-                group_e(n - 2)
             if 0 <= n - 3 < TILES:
                 quantise_e(n - 3)
-            if 0 <= n - 8 < TILES and (n - 8) % T == T - 1:
+            if last_tile_of_group(n - 5):
+                invert_row_sums((n - 5) // T)
+            if last_tile_of_group(n - 8):
                 divide_and_store((n - 8) // T)
+            if 0 <= n - 2 < TILES:
+                group_e(n - 2)
+
+        def step_end(n):
+            if 0 <= n + 1 < TILES:
+                scale_maximum(n + 1)
+            if 0 <= n < TILES:
+                exponent(n)
 
         for b in range(-1, B + 1):
             first = b * TILES_PER_BATCH
-            finish = 1 <= b < B
-            prepare = 0 <= b < B - 1
-            step(first)
+            finish = 0 <= b < B
+            transposes = 0 <= b < B - 1
+            values = -1 <= b < B - 1
+            step_begin(first)
             if finish:
                 copy_values(b, 1, waiting["v1"])
-            if prepare:
+            if transposes:
                 waiting["q"] = transpose_heads(q_in[b + 1])
-            step(first + 1)
+            step_end(first)
+            step_begin(first + 1)
             if finish:
                 quantise_values(b)
-            if prepare:
+            if transposes:
                 q_t[b + 1] = copy_heads(waiting["q"], "q_t", True)
                 waiting["k"] = transpose_heads(k_in[b + 1])
-            step(first + 2)
-            if prepare:
+            step_end(first + 1)
+            step_begin(first + 2)
+            if transposes:
                 k_t[b + 1] = copy_heads(waiting["k"], "k_t", True)
                 waiting["x0"] = transpose_x(b + 1, 0)
-            step(first + 3)
-            if prepare:
+            step_end(first + 2)
+            step_begin(first + 3)
+            if transposes:
                 copy_x(b + 1, 0, waiting["x0"])
                 waiting["x1"] = transpose_x(b + 1, 1)
-            step(first + 4)
-            if prepare:
+            step_end(first + 3)
+            step_begin(first + 4)
+            if transposes:
                 copy_x(b + 1, 1, waiting["x1"])
-            step(first + 5)
-            if prepare:
+            step_end(first + 4)
+            step_begin(first + 5)
+            if transposes:
                 quantise_x(b + 1)
-            step(first + 6)
-            if prepare:
+            step_end(first + 5)
+            step_begin(first + 6)
+            if values:
                 waiting["v0"] = project_values(b + 1, 0)
                 waiting["v1"] = project_values(b + 1, 1)
-            step(first + 7)
-            if prepare:
+            step_end(first + 6)
+            step_begin(first + 7)
+            if values:
                 copy_values(b + 1, 0, waiting["v0"])
+            step_end(first + 7)

@@ -191,7 +191,10 @@ def tile_bayesianattention_pa_t_kernel(tc, x, wv, q, k, mask, shape, scale, loc,
             if h == 0:
                 grouped = batch.tile([P, H, HD, T], BF16, tag="v_grouped", align_bytes=64)
                 v_grouped[b] = grouped
-            nc.vector.tensor_copy(out=v_grouped[b][:, h, :, :], in_=v_ps[:].rearrange("p t d -> p d t"))
+            if b == 0:
+                nc.scalar.copy(out=v_grouped[b][:, h, :, :], in_=v_ps[:].rearrange("p t d -> p d t"))
+            else:
+                nc.vector.tensor_copy(out=v_grouped[b][:, h, :, :], in_=v_ps[:].rearrange("p t d -> p d t"))
 
         def quantise_values(b):
             codes = batch.tile([P, E], U32, tag="v_codes", align_bytes=64)
@@ -286,10 +289,13 @@ def tile_bayesianattention_pa_t_kernel(tc, x, wv, q, k, mask, shape, scale, loc,
                 out=row_max[g][:, ti : ti + 1], in_=s_banks[n][:].rearrange("p t j -> p (t j)"), axis=AXIS.X
             )
 
-        def scale_maximum(n):
-            g, ti = divmod(n, T)
-            nc.vector.tensor_scalar_mul(
-                out=exp_bias[g][:, ti : ti + 1], in0=row_max[g][:, ti : ti + 1], scalar1=-1.0 / math.sqrt(HD)
+            nc.gpsimd.tensor_scalar(
+                out=exp_bias[g][:, ti : ti + 1],
+                in0=row_max[g][:, ti : ti + 1],
+                scalar1=-1.0 / math.sqrt(HD),
+                scalar2=0.0,
+                op0=ALU.mult,
+                op1=ALU.add,
             )
 
         def exponent(n):
@@ -388,8 +394,6 @@ def tile_bayesianattention_pa_t_kernel(tc, x, wv, q, k, mask, shape, scale, loc,
                 group_e(n - 2)
 
         def step_end(n):
-            if 0 <= n + 1 < TILES:
-                scale_maximum(n + 1)
             if 0 <= n < TILES:
                 exponent(n)
 
@@ -408,7 +412,7 @@ def tile_bayesianattention_pa_t_kernel(tc, x, wv, q, k, mask, shape, scale, loc,
             if finish:
                 quantise_values(b)
             if transposes:
-                q_t[b + 1] = copy_heads(waiting["q"], "q_t", True)
+                q_t[b + 1] = copy_heads(waiting["q"], "q_t", False)
                 waiting["k"] = transpose_heads(k_in[b + 1])
             step_end(first + 1)
             step_begin(first + 2)

@@ -303,10 +303,10 @@ def tile_bayesianattention_pa_t_kernel(tc, x, wv, q, k, mask, shape, scale, loc,
             if ti == 0:
                 sums = group.tile([P, T], F32, tag="row_sum")
                 row_sum[g] = sums
-            e_sb = rows.tile([P, T, P], BF16, tag="e")
+            e_sb = rows.tile([P, 2, P, 2], BF16, tag="e")
             nc.scalar.activation(
-                out=e_sb[:].rearrange("p t j -> p (t j)"),
-                in_=s_banks[n][:].rearrange("p t j -> p (t j)"),
+                out=e_sb[:],
+                in_=s_banks[n][:].rearrange("p (u w) j -> p u j w", u=2),
                 func=ACT.Exp,
                 scale=1.0 / math.sqrt(HD),
                 bias=exp_bias[g][:, ti : ti + 1],
@@ -315,14 +315,18 @@ def tile_bayesianattention_pa_t_kernel(tc, x, wv, q, k, mask, shape, scale, loc,
             e_rows[n] = e_sb
 
         def transpose_e(n):
-            e_ps = psum_et.tile([P, T, P], BF16, tag="et")
-            for t in range(T):
-                nc.tensor.transpose(e_ps[:, t, :], e_rows[n][:, t, :], ident_bf[:])
+            e_ps = psum_et.tile([P, 2, P], F32, tag="et")
+            e_words = e_rows[n][:].rearrange("p u j w -> p (u j w)").bitcast(F32)
+            for u in range(2):
+                nc.tensor.transpose(e_ps[:, u, :], e_words[:, u * P : (u + 1) * P], ident_f32[:])
             e_banks[n] = e_ps
 
         def group_e(n):
             e_grouped = rows.tile([P, P, T], BF16, tag="e_grouped", align_bytes=64)
-            nc.scalar.copy(out=e_grouped[:], in_=e_banks[n][:].rearrange("p t i -> p i t"))
+            nc.scalar.copy(
+                out=e_grouped[:].rearrange("p i t -> p (i t)").bitcast(F32).rearrange("p (i u) -> p i u", u=2),
+                in_=e_banks[n][:].rearrange("p u i -> p i u"),
+            )
             e_groups[n] = e_grouped
 
         def quantise_e(n):

@@ -31,13 +31,12 @@ def tile_bayesianattention_pa_t_kernel(tc, x, wv, q, k, mask, shape, scale, loc,
         ctx.enter_context(tc.manual_schedule())
         const = ctx.enter_context(tc.tile_pool(name="const", bufs=1))
         inputs = ctx.enter_context(tc.tile_pool(name="inputs", bufs=B))
-        batch = ctx.enter_context(tc.tile_pool(name="batch", bufs=2))
+        batch = ctx.enter_context(tc.tile_pool(name="batch", bufs=3))
         group = ctx.enter_context(tc.tile_pool(name="group", bufs=4))
-        rows = ctx.enter_context(tc.tile_pool(name="rows", bufs=3))
-        psum_prep = ctx.enter_context(tc.psum_pool(name="psum_prep", bufs=2))
-        psum_s = ctx.enter_context(tc.psum_pool(name="psum_s", bufs=3))
+        rows = ctx.enter_context(tc.tile_pool(name="rows", bufs=8))
+        psum_s = ctx.enter_context(tc.psum_pool(name="psum_s", bufs=4))
         psum_et = ctx.enter_context(tc.psum_pool(name="psum_et", bufs=2))
-        psum_o = ctx.enter_context(tc.psum_pool(name="psum_o", bufs=1))
+        psum_misc = ctx.enter_context(tc.psum_pool(name="psum_misc", bufs=2))
 
         def load_parameter(param, name):
             row = const.tile([P, H], BF16, name=name)
@@ -132,49 +131,50 @@ def tile_bayesianattention_pa_t_kernel(tc, x, wv, q, k, mask, shape, scale, loc,
         v_grouped, v_codes, v_scales = {}, {}, {}
 
         def transpose_heads(src):
-            t_ps = psum_prep.tile([P, H, T, P], BF16, tag="prep")
+            t_ps = psum_misc.tile([P, H, T, P], BF16, tag="misc")
             for h in range(H):
                 for t in range(T):
                     nc.tensor.transpose(t_ps[:, h, t, :], src[:, t, h * HD : (h + 1) * HD], ident_bf[:])
             return t_ps
 
-        def copy_heads(t_ps, tag, on_scalar):
+        def copy_heads(t_ps, tag):
             t_sb = batch.tile([P, H, T, P], BF16, tag=tag)
-            if on_scalar:
-                nc.scalar.copy(out=t_sb[:], in_=t_ps[:])
-            else:
-                nc.vector.tensor_copy(out=t_sb[:], in_=t_ps[:])
+            nc.vector.tensor_copy(out=t_sb[:], in_=t_ps[:])
             return t_sb
 
         def transpose_x(b, half):
-            x_ps = psum_prep.tile([P, 2, 2, P], F32, tag="prep")
+            x_ps = psum_misc.tile([P, 2, 2, P], F32, tag="misc")
             for t2 in range(2):
                 x_words = x_in[b][:, 2 * half + t2, :].bitcast(F32)
                 for u in range(2):
                     nc.tensor.transpose(x_ps[:, t2, u, :], x_words[:, u * P : (u + 1) * P], ident_f32[:])
             return x_ps
 
-        def copy_x(b, half, x_ps):
+        def copy_x(b, half, x_ps, on_scalar=True):
             if half == 0:
                 grouped = batch.tile([P, T, P, T], BF16, tag="x_grouped", align_bytes=64)
                 x_grouped[b] = grouped
-            nc.vector.tensor_copy(
-                out=x_grouped[b][:, 2 * half : 2 * half + 2, :, :].bitcast(F32),
-                in_=x_ps[:].rearrange("p t u r -> p t r u"),
-            )
+            dst = x_grouped[b][:, 2 * half : 2 * half + 2, :, :].bitcast(F32)
+            src = x_ps[:].rearrange("p t u r -> p t r u")
+            if on_scalar:
+                nc.scalar.copy(out=dst, in_=src)
+            else:
+                nc.vector.tensor_copy(out=dst, in_=src)
 
-        def quantise_x(b):
-            codes = batch.tile([P, T * P], U32, tag="x_codes", align_bytes=64)
-            scales = batch.tile([P, T * P], U8, tag="x_scales", align_bytes=64)
+        def quantise_x(b, half):
+            if half == 0:
+                codes = batch.tile([P, T * P], U32, tag="x_codes", align_bytes=64)
+                scales = batch.tile([P, T * P], U8, tag="x_scales", align_bytes=64)
+                x_codes[b], x_scales[b] = codes, scales
+            cols = slice(half * 2 * P, (half + 1) * 2 * P)
             nc.vector.quantize_mx(
-                out=codes[:].bitcast(FP8X4),
-                scales=scales[:],
-                in_=x_grouped[b][:].rearrange("p t r w -> p (t r w)"),
+                out=x_codes[b][:, cols].bitcast(FP8X4),
+                scales=x_scales[b][:, cols],
+                in_=x_grouped[b][:, 2 * half : 2 * half + 2, :, :].rearrange("p t r w -> p (t r w)"),
             )
-            x_codes[b], x_scales[b] = codes, scales
 
         def project_values(b, h):
-            v_ps = psum_prep.tile([P, T, HD], F32, tag="prep")
+            v_ps = psum_misc.tile([P, T, HD], F32, tag="misc")
             for t in range(T):
                 nc.tensor.matmul_mx(
                     out=v_ps[:, t, :],
@@ -191,10 +191,7 @@ def tile_bayesianattention_pa_t_kernel(tc, x, wv, q, k, mask, shape, scale, loc,
             if h == 0:
                 grouped = batch.tile([P, H, HD, T], BF16, tag="v_grouped", align_bytes=64)
                 v_grouped[b] = grouped
-            if b == 0:
-                nc.scalar.copy(out=v_grouped[b][:, h, :, :], in_=v_ps[:].rearrange("p t d -> p d t"))
-            else:
-                nc.vector.tensor_copy(out=v_grouped[b][:, h, :, :], in_=v_ps[:].rearrange("p t d -> p d t"))
+            nc.scalar.copy(out=v_grouped[b][:, h, :, :], in_=v_ps[:].rearrange("p t d -> p d t"))
 
         def quantise_values(b):
             codes = batch.tile([P, E], U32, tag="v_codes", align_bytes=64)
@@ -208,13 +205,13 @@ def tile_bayesianattention_pa_t_kernel(tc, x, wv, q, k, mask, shape, scale, loc,
 
         q_ps = transpose_heads(q_in[0])
         k_ps = transpose_heads(k_in[0])
-        q_t[0] = copy_heads(q_ps, "q_t", False)
-        k_t[0] = copy_heads(k_ps, "k_t", False)
+        q_t[0] = copy_heads(q_ps, "q_t")
+        k_t[0] = copy_heads(k_ps, "k_t")
         wv_grouped = const.tile([P, E, T], BF16, align_bytes=64)
         nc.vector.tensor_copy(out=wv_grouped[:], in_=wv_sb[:].rearrange("p t c -> p c t"))
         x_low = transpose_x(0, 0)
         x_high = transpose_x(0, 1)
-        copy_x(0, 0, x_low)
+        copy_x(0, 0, x_low, False)
         wv_codes = const.tile([P, E], U32, align_bytes=64)
         wv_scales = const.tile([P, E], U8, align_bytes=64)
         nc.vector.quantize_mx(
@@ -222,14 +219,14 @@ def tile_bayesianattention_pa_t_kernel(tc, x, wv, q, k, mask, shape, scale, loc,
             scales=wv_scales[:],
             in_=wv_grouped[:].rearrange("p c t -> p (c t)"),
         )
-        copy_x(0, 1, x_high)
+        copy_x(0, 1, x_high, False)
         mask_rows = const.tile([P, T, T, P], BF16)
         nc.vector.tensor_copy(out=mask_rows[:], in_=mask_sb[:].rearrange("p a (j t) -> p a t j", t=T))
-        quantise_x(0)
+        quantise_x(0, 0)
         mask_t = const.tile([P, T, T, P], BF16)
         mask_banks = []
         for half in range(2):
-            mask_ps = psum_prep.tile([P, 2, T, P], BF16, tag="prep")
+            mask_ps = psum_misc.tile([P, 2, T, P], BF16, tag="misc")
             mask_banks.append(mask_ps)
             for ti2 in range(2):
                 for t in range(T):
@@ -238,6 +235,9 @@ def tile_bayesianattention_pa_t_kernel(tc, x, wv, q, k, mask, shape, scale, loc,
                     )
         for half in range(2):
             nc.vector.tensor_copy(out=mask_t[:, 2 * half : 2 * half + 2, :, :], in_=mask_banks[half][:])
+        quantise_x(0, 1)
+        k_ps = transpose_heads(k_in[1])
+        k_t[1] = copy_heads(k_ps, "k_t")
 
         added = []
         for h in range(H):
@@ -257,7 +257,7 @@ def tile_bayesianattention_pa_t_kernel(tc, x, wv, q, k, mask, shape, scale, loc,
                 op1=ALU.subtract,
             )
 
-        def scores(n):
+        def multiply_queries_and_keys(n):
             g, ti = divmod(n, T)
             b, h = divmod(g, H)
             s_ps = psum_s.tile([P, T, P], F32, tag="s")
@@ -268,16 +268,20 @@ def tile_bayesianattention_pa_t_kernel(tc, x, wv, q, k, mask, shape, scale, loc,
                 start=True,
                 stop=False,
             )
+            s_banks[n] = s_ps
+
+        def add_bias_to_scores(n):
+            g, ti = divmod(n, T)
+            h = g % H
             for t in range(T):
                 nc.tensor.matmul(
-                    out=s_ps[:, t, :],
+                    out=s_banks[n][:, t, :],
                     lhsT=added[h][:, ti, t, :],
                     rhs=ident_f32[:],
                     is_transpose=True,
                     start=False,
                     stop=(t == T - 1),
                 )
-            s_banks[n] = s_ps
 
         def row_maximum(n):
             g, ti = divmod(n, T)
@@ -314,36 +318,37 @@ def tile_bayesianattention_pa_t_kernel(tc, x, wv, q, k, mask, shape, scale, loc,
             )
             e_rows[n] = e_sb
 
-        def transpose_e(n):
-            e_ps = psum_et.tile([P, 2, P], F32, tag="et")
-            e_words = e_rows[n][:].rearrange("p u j w -> p (u j w)").bitcast(F32)
-            for u in range(2):
-                nc.tensor.transpose(e_ps[:, u, :], e_words[:, u * P : (u + 1) * P], ident_f32[:])
-            e_banks[n] = e_ps
+        def transpose_e(m):
+            e_ps = psum_et.tile([P, 2, 2, P], F32, tag="et")
+            for i in range(2):
+                e_words = e_rows[2 * m + i][:].rearrange("p u j w -> p (u j w)").bitcast(F32)
+                for u in range(2):
+                    nc.tensor.transpose(e_ps[:, i, u, :], e_words[:, u * P : (u + 1) * P], ident_f32[:])
+            e_banks[m] = e_ps
 
-        def group_e(n):
-            e_grouped = rows.tile([P, P, T], BF16, tag="e_grouped", align_bytes=64)
+        def group_e(m):
+            g, half = divmod(m, 2)
+            if half == 0:
+                grouped = group.tile([P, T, P, T], BF16, tag="e_grouped", align_bytes=64)
+                e_groups[g] = grouped
             nc.scalar.copy(
-                out=e_grouped[:].rearrange("p i t -> p (i t)").bitcast(F32).rearrange("p (i u) -> p i u", u=2),
-                in_=e_banks[n][:].rearrange("p u i -> p i u"),
+                out=e_groups[g][:, 2 * half : 2 * half + 2, :, :].bitcast(F32),
+                in_=e_banks[m][:].rearrange("p a u i -> p a i u"),
             )
-            e_groups[n] = e_grouped
 
-        def quantise_e(n):
-            g, ti = divmod(n, T)
-            if ti == 0:
-                codes = group.tile([P, T * P], U32, tag="e_codes", align_bytes=64)
-                scales = group.tile([P, T * P], U8, tag="e_scales", align_bytes=64)
-                e_codes[g], e_scales[g] = codes, scales
+        def quantise_e(g):
+            codes = group.tile([P, T * P], U32, tag="e_codes", align_bytes=64)
+            scales = group.tile([P, T * P], U8, tag="e_scales", align_bytes=64)
+            e_codes[g], e_scales[g] = codes, scales
             nc.vector.quantize_mx(
-                out=e_codes[g][:, ti * P : (ti + 1) * P].bitcast(FP8X4),
-                scales=e_scales[g][:, ti * P : (ti + 1) * P],
-                in_=e_groups[n][:].rearrange("p i t -> p (i t)"),
+                out=codes[:].bitcast(FP8X4),
+                scales=scales[:],
+                in_=e_groups[g][:].rearrange("p a i t -> p (a i t)"),
             )
 
         def attend(g):
             b, h = divmod(g, H)
-            o_ps = psum_o.tile([P, T, HD], F32, tag="o_ps")
+            o_ps = psum_misc.tile([P, T, HD], F32, tag="misc")
             for ti in range(T):
                 nc.tensor.matmul_mx(
                     out=o_ps[:, ti, :],
@@ -374,75 +379,66 @@ def tile_bayesianattention_pa_t_kernel(tc, x, wv, q, k, mask, shape, scale, loc,
                 out=out[b].rearrange("(p t) c -> p t c", t=T)[:, :, h * HD : (h + 1) * HD], in_=o_sb[:]
             )
 
-        def last_tile_of_group(n):
-            return 0 <= n < TILES and n % T == T - 1
+        for n in range(-4, TILES + TILES_PER_BATCH):
+            b, j = divmod(n, TILES_PER_BATCH)
+            g1, g0 = (b - 1) * H + 1, b * H
 
-        def step_begin(n):
-            if 0 <= n + 1 < TILES:
-                row_maximum(n + 1)
-            if 0 <= n + 3 < TILES_PER_BATCH:
-                add_prior_and_mask(n + 3)
-            if 0 <= n - 1 < TILES:
-                transpose_e(n - 1)
+            if 0 <= n + 4 < TILES_PER_BATCH:
+                add_prior_and_mask(n + 4)
             if 0 <= n + 2 < TILES:
-                scores(n + 2)
-            if last_tile_of_group(n - 7):
-                attend((n - 7) // T)
-            if 0 <= n - 3 < TILES:
-                quantise_e(n - 3)
-            if last_tile_of_group(n - 5):
-                invert_row_sums((n - 5) // T)
-            if last_tile_of_group(n - 8):
-                divide_and_store((n - 8) // T)
-            if 0 <= n - 2 < TILES:
-                group_e(n - 2)
+                row_maximum(n + 2)
+            if j == 0:
+                if 1 <= b < B:
+                    quantise_x(b, 1)
+                if b >= 1:
+                    invert_row_sums(g1)
+            elif j == 1 and b < B - 1:
+                q_t[b + 1] = copy_heads(waiting["q"], "q_t")
+            elif j == 2 and b >= 1:
+                divide_and_store(g1 - 1)
+            elif j == 3 and b >= 1:
+                quantise_e(g1)
+            elif j == 4 and 0 <= b < B:
+                if b < B - 1:
+                    quantise_x(b + 1, 0)
+                invert_row_sums(g0)
+            elif j == 5 and 0 <= b < B - 2:
+                k_t[b + 2] = copy_heads(waiting["k"], "k_t")
+            elif j == 6 and b >= 1:
+                divide_and_store(g1)
+            elif j == 7 and 0 <= b < B:
+                quantise_e(g0)
 
-        def step_end(n):
+            if j in (0, 1) and b >= 1:
+                transpose_e(2 * g1 + j)
+            elif j in (4, 5) and 0 <= b < B:
+                transpose_e(2 * g0 + j - 4)
+            if j == 0 and b < B - 1:
+                waiting["q"] = transpose_heads(q_in[b + 1])
+            elif j == 4 and 0 <= b < B - 2:
+                waiting["k"] = transpose_heads(k_in[b + 2])
+            elif j in (2, 6) and 0 <= b < B - 1:
+                waiting["x", j // 4] = transpose_x(b + 1, j // 4)
+            if 0 <= n + 3 < TILES:
+                multiply_queries_and_keys(n + 3)
+            if j in (1, 5) and b >= 1:
+                attend(g1 - 1 + j // 4)
+            elif j in (3, 7) and 0 <= b < B:
+                waiting["v", j // 4] = project_values(b, j // 4)
+            if 0 <= n + 3 < TILES:
+                add_bias_to_scores(n + 3)
+
+            if j == 0 and b >= 1:
+                copy_values(b - 1, 1, waiting["v", 1])
+            elif j == 4 and 0 <= b < B:
+                copy_values(b, 0, waiting["v", 0])
+            elif j in (1, 2) and b >= 1:
+                group_e(2 * g1 + j - 1)
+            elif j in (5, 6) and 0 <= b < B:
+                group_e(2 * g0 + j - 5)
+            elif j in (3, 7) and 0 <= b < B - 1:
+                copy_x(b + 1, j // 4, waiting["x", j // 4])
             if 0 <= n < TILES:
                 exponent(n)
-
-        for b in range(-1, B + 1):
-            first = b * TILES_PER_BATCH
-            finish = 0 <= b < B
-            transposes = 0 <= b < B - 1
-            values = -1 <= b < B - 1
-            step_begin(first)
-            if finish:
-                copy_values(b, 1, waiting["v1"])
-            if transposes:
-                waiting["q"] = transpose_heads(q_in[b + 1])
-            step_end(first)
-            step_begin(first + 1)
-            if finish:
-                quantise_values(b)
-            if transposes:
-                q_t[b + 1] = copy_heads(waiting["q"], "q_t", False)
-                waiting["k"] = transpose_heads(k_in[b + 1])
-            step_end(first + 1)
-            step_begin(first + 2)
-            if transposes:
-                k_t[b + 1] = copy_heads(waiting["k"], "k_t", True)
-                waiting["x0"] = transpose_x(b + 1, 0)
-            step_end(first + 2)
-            step_begin(first + 3)
-            if transposes:
-                copy_x(b + 1, 0, waiting["x0"])
-                waiting["x1"] = transpose_x(b + 1, 1)
-            step_end(first + 3)
-            step_begin(first + 4)
-            if transposes:
-                copy_x(b + 1, 1, waiting["x1"])
-            step_end(first + 4)
-            step_begin(first + 5)
-            if transposes:
-                quantise_x(b + 1)
-            step_end(first + 5)
-            step_begin(first + 6)
-            if values:
-                waiting["v0"] = project_values(b + 1, 0)
-                waiting["v1"] = project_values(b + 1, 1)
-            step_end(first + 6)
-            step_begin(first + 7)
-            if values:
-                copy_values(b + 1, 0, waiting["v0"])
-            step_end(first + 7)
+            if j == 0 and b >= 1:
+                quantise_values(b - 1)

@@ -20,7 +20,6 @@ P = 128
 T = 4
 TILES = B * H * T
 TILES_PER_BATCH = H * T
-OFFSETS = 2 * T - 1
 
 FLOPS = 2 * B * S * D * E + 2 * 2 * B * H * S * S * HD
 
@@ -64,6 +63,8 @@ def tile_bayesianattention_pa_t_kernel(tc, x, wv, q, k, mask, shape, scale, loc,
             x_in[b] = x_sb
 
         load_queries_and_keys(0)
+        mask_sb = const.tile([P, T, S], BF16)
+        nc.sync.dma_start(out=mask_sb[:], in_=mask[0, 0].rearrange("(p t) j -> p t j", t=T))
         wv_sb = const.tile([P, T, E], BF16)
         for u in range(2):
             nc.sync.dma_start(
@@ -71,32 +72,23 @@ def tile_bayesianattention_pa_t_kernel(tc, x, wv, q, k, mask, shape, scale, loc,
                 in_=wv[2 * P * u : 2 * P * (u + 1), :].rearrange("(p e) c -> p e c", e=2),
             )
         load_x(0)
-        mask_sb = const.tile([P, T, S], BF16)
-        nc.sync.dma_start(out=mask_sb[:], in_=mask[0, 0].rearrange("(p t) j -> p t j", t=T))
         for b in range(1, B):
             load_queries_and_keys(b)
             load_x(b)
 
         ident_bf = const.tile([P, P], BF16)
         make_identity(nc, ident_bf[:])
-        dist_partitions = const.tile([P, P], F32)
+        dist = const.tile([P, T, P + 1], F32)
         nc.gpsimd.iota(
-            dist_partitions[:], pattern=[[-T, P]], base=0, channel_multiplier=T,
-            allow_small_or_imprecise_dtypes=True,
-        )
-        dist_rows = const.tile([P, OFFSETS], F32)
-        nc.gpsimd.iota(
-            dist_rows[:], pattern=[[1, OFFSETS]], base=1 - T, channel_multiplier=0,
+            dist[:], pattern=[[1, T], [-T, P + 1]], base=1, channel_multiplier=T,
             allow_small_or_imprecise_dtypes=True,
         )
         ident_f32 = const.tile([P, P], F32)
         make_identity(nc, ident_f32[:])
-        dist = const.tile([P, OFFSETS, P], F32)
-        nc.vector.tensor_tensor(
-            out=dist[:],
-            in0=dist_partitions[:].unsqueeze(1).to_broadcast([P, OFFSETS, P]),
-            in1=dist_rows[:].unsqueeze(2).to_broadcast([P, OFFSETS, P]),
-            op=ALU.add,
+        wv_grouped = const.tile([P, E, T], BF16, align_bytes=64)
+        nc.gpsimd.tensor_scalar(
+            out=wv_grouped[:], in0=wv_sb[:].rearrange("p t c -> p c t"),
+            scalar1=1.0, scalar2=0.0, op0=ALU.mult, op1=ALU.add,
         )
 
         slope = const.tile([P, H], F32)
@@ -105,6 +97,8 @@ def tile_bayesianattention_pa_t_kernel(tc, x, wv, q, k, mask, shape, scale, loc,
         nc.scalar.activation(out=exp_loc[:], in_=loc_bf[:], func=ACT.Exp)
         exp_neg_loc = const.tile([P, H], F32)
         nc.scalar.activation(out=exp_neg_loc[:], in_=loc_bf[:], func=ACT.Exp, scale=-1.0)
+        ln_table = const.tile([P, 1], F32)
+        nc.scalar.activation(out=ln_table[:], in_=slope[:, :1], func=ACT.Ln)
         shift = const.tile([P, H], F32)
         nc.vector.tensor_sub(out=shift[:], in0=exp_neg_loc[:], in1=exp_loc[:])
         nc.vector.tensor_mul(out=shift[:], in0=shift[:], in1=slope[:])
@@ -112,7 +106,7 @@ def tile_bayesianattention_pa_t_kernel(tc, x, wv, q, k, mask, shape, scale, loc,
         nc.vector.tensor_copy(out=power[:], in_=shape_bf[:])
         prior = []
         for h in range(H):
-            prior_h = const.tile([P, OFFSETS, P], F32, name="prior%d" % h)
+            prior_h = const.tile([P, T, P + 1], F32, name="prior%d" % h)
             prior.append(prior_h)
             nc.scalar.activation(
                 out=prior_h[:], in_=dist[:], func=ACT.Abs,
@@ -130,8 +124,8 @@ def tile_bayesianattention_pa_t_kernel(tc, x, wv, q, k, mask, shape, scale, loc,
         q_t, k_t, x_grouped, x_codes, x_scales = {}, {}, {}, {}, {}
         v_grouped, v_codes, v_scales = {}, {}, {}
 
-        def transpose_heads(src):
-            t_ps = psum_misc.tile([P, H, T, P], BF16, tag="misc")
+        def transpose_heads(src, pool=psum_misc, tag="misc"):
+            t_ps = pool.tile([P, H, T, P], BF16, tag=tag)
             for h in range(H):
                 for t in range(T):
                     nc.tensor.transpose(t_ps[:, h, t, :], src[:, t, h * HD : (h + 1) * HD], ident_bf[:])
@@ -142,8 +136,8 @@ def tile_bayesianattention_pa_t_kernel(tc, x, wv, q, k, mask, shape, scale, loc,
             nc.vector.tensor_copy(out=t_sb[:], in_=t_ps[:])
             return t_sb
 
-        def transpose_x(b, half):
-            x_ps = psum_misc.tile([P, 2, 2, P], F32, tag="misc")
+        def transpose_x(b, half, pool=psum_misc, tag="misc"):
+            x_ps = pool.tile([P, 2, 2, P], F32, tag=tag)
             for t2 in range(2):
                 x_words = x_in[b][:, 2 * half + t2, :].bitcast(F32)
                 for u in range(2):
@@ -203,15 +197,36 @@ def tile_bayesianattention_pa_t_kernel(tc, x, wv, q, k, mask, shape, scale, loc,
             )
             v_codes[b], v_scales[b] = codes, scales
 
+        mask_t = const.tile([P, T, T, P], F32)
+
+        def transpose_mask(half):
+            mask_ps = psum_et.tile([P, 2, 2, P], F32, tag="et")
+            for ti2 in range(2):
+                words = mask_sb[:, 2 * half + ti2, :].bitcast(F32).rearrange("p (j u) -> p u j", u=2)
+                for u in range(2):
+                    nc.tensor.transpose(mask_ps[:, ti2, u, :], words[:, u, :], ident_f32[:])
+            return mask_ps
+
+        def scale_mask(half, mask_ps):
+            for ti2 in range(2):
+                nc.vector.tensor_scalar(
+                    out=mask_t[:, 2 * half + ti2, :, :].rearrange("p (u w) i -> p u w i", u=2),
+                    in0=mask_ps[:, ti2, :, :].bitcast(BF16).rearrange("p u (i w) -> p u w i", w=2),
+                    scalar1=math.sqrt(HD), scalar2=0.0, op0=ALU.mult, op1=ALU.add,
+                )
+
         q_ps = transpose_heads(q_in[0])
         k_ps = transpose_heads(k_in[0])
         q_t[0] = copy_heads(q_ps, "q_t")
         k_t[0] = copy_heads(k_ps, "k_t")
-        wv_grouped = const.tile([P, E, T], BF16, align_bytes=64)
-        nc.vector.tensor_copy(out=wv_grouped[:], in_=wv_sb[:].rearrange("p t c -> p c t"))
+        mask_banks = [transpose_mask(0), transpose_mask(1)]
+        scale_mask(0, mask_banks[0])
+        scale_mask(1, mask_banks[1])
         x_low = transpose_x(0, 0)
         x_high = transpose_x(0, 1)
         copy_x(0, 0, x_low, False)
+        copy_x(0, 1, x_high)
+        quantise_x(0, 0)
         wv_codes = const.tile([P, E], U32, align_bytes=64)
         wv_scales = const.tile([P, E], U8, align_bytes=64)
         nc.vector.quantize_mx(
@@ -219,25 +234,12 @@ def tile_bayesianattention_pa_t_kernel(tc, x, wv, q, k, mask, shape, scale, loc,
             scales=wv_scales[:],
             in_=wv_grouped[:].rearrange("p c t -> p (c t)"),
         )
-        copy_x(0, 1, x_high, False)
-        mask_rows = const.tile([P, T, T, P], BF16)
-        nc.vector.tensor_copy(out=mask_rows[:], in_=mask_sb[:].rearrange("p a (j t) -> p a t j", t=T))
-        quantise_x(0, 0)
-        mask_t = const.tile([P, T, T, P], BF16)
-        mask_banks = []
-        for half in range(2):
-            mask_ps = psum_misc.tile([P, 2, T, P], BF16, tag="misc")
-            mask_banks.append(mask_ps)
-            for ti2 in range(2):
-                for t in range(T):
-                    nc.tensor.transpose(
-                        mask_ps[:, ti2, t, :], mask_rows[:, 2 * half + ti2, t, :], ident_bf[:]
-                    )
-        for half in range(2):
-            nc.vector.tensor_copy(out=mask_t[:, 2 * half : 2 * half + 2, :, :], in_=mask_banks[half][:])
-        quantise_x(0, 1)
-        k_ps = transpose_heads(k_in[1])
-        k_t[1] = copy_heads(k_ps, "k_t")
+        warm_ps = psum_s.tile([P, T, P], F32, tag="s")
+        for i in range(8):
+            nc.tensor.matmul(
+                out=warm_ps[:].rearrange("p t j -> p (t j)"), lhsT=ident_bf[:],
+                rhs=k_t[0][:, 0, :, :].rearrange("p t j -> p (t j)"), start=True, stop=True,
+            )
 
         added = []
         for h in range(H):
@@ -248,14 +250,20 @@ def tile_bayesianattention_pa_t_kernel(tc, x, wv, q, k, mask, shape, scale, loc,
 
         def add_prior_and_mask(n):
             h, ti = divmod(n, T)
-            nc.vector.scalar_tensor_tensor(
-                out=added[h][:, ti, :, :],
-                in0=mask_t[:, ti, :, :],
-                scalar=math.sqrt(HD),
-                in1=prior[h][:, T - 1 - ti : 2 * T - 1 - ti, :],
-                op0=ALU.mult,
-                op1=ALU.subtract,
+            engine = nc.vector
+            engine.tensor_tensor(
+                out=added[h][:, ti, : ti + 1, :],
+                in0=mask_t[:, ti, : ti + 1, :],
+                in1=prior[h][:, T - 1 - ti :, 1:],
+                op=ALU.subtract,
             )
+            if ti < T - 1:
+                engine.tensor_tensor(
+                    out=added[h][:, ti, ti + 1 :, :],
+                    in0=mask_t[:, ti, ti + 1 :, :],
+                    in1=prior[h][:, : T - 1 - ti, :P],
+                    op=ALU.subtract,
+                )
 
         def multiply_queries_and_keys(n):
             g, ti = divmod(n, T)
@@ -318,127 +326,201 @@ def tile_bayesianattention_pa_t_kernel(tc, x, wv, q, k, mask, shape, scale, loc,
             )
             e_rows[n] = e_sb
 
-        def transpose_e(m):
-            e_ps = psum_et.tile([P, 2, 2, P], F32, tag="et")
-            for i in range(2):
-                e_words = e_rows[2 * m + i][:].rearrange("p u j w -> p (u j w)").bitcast(F32)
+        def transpose_e(first, count=2, pool=psum_et, tag="et"):
+            e_ps = pool.tile([P, count, 2, P], F32, tag=tag)
+            for i in range(count):
+                e_words = e_rows[first + i][:].rearrange("p u j w -> p (u j w)").bitcast(F32)
                 for u in range(2):
                     nc.tensor.transpose(e_ps[:, i, u, :], e_words[:, u * P : (u + 1) * P], ident_f32[:])
-            e_banks[m] = e_ps
+            e_banks[first] = e_ps
 
-        def group_e(m):
-            g, half = divmod(m, 2)
-            if half == 0:
+        def group_e(first, count=2, copy=nc.scalar.copy):
+            g, ti = divmod(first, T)
+            if ti == 0:
                 grouped = group.tile([P, T, P, T], BF16, tag="e_grouped", align_bytes=64)
                 e_groups[g] = grouped
-            nc.scalar.copy(
-                out=e_groups[g][:, 2 * half : 2 * half + 2, :, :].bitcast(F32),
-                in_=e_banks[m][:].rearrange("p a u i -> p a i u"),
+            copy(
+                out=e_groups[g][:, ti : ti + count, :, :].bitcast(F32),
+                in_=e_banks[first][:].rearrange("p a u i -> p a i u"),
             )
 
-        def quantise_e(g):
-            codes = group.tile([P, T * P], U32, tag="e_codes", align_bytes=64)
-            scales = group.tile([P, T * P], U8, tag="e_scales", align_bytes=64)
-            e_codes[g], e_scales[g] = codes, scales
+        def quantise_e(g, first=0, count=T):
+            if first == 0:
+                codes = group.tile([P, T * P], U32, tag="e_codes", align_bytes=64)
+                scales = group.tile([P, T * P], U8, tag="e_scales", align_bytes=64)
+                e_codes[g], e_scales[g] = codes, scales
+            cols = slice(first * P, (first + count) * P)
             nc.vector.quantize_mx(
-                out=codes[:].bitcast(FP8X4),
-                scales=scales[:],
-                in_=e_groups[g][:].rearrange("p a i t -> p (a i t)"),
+                out=e_codes[g][:, cols].bitcast(FP8X4),
+                scales=e_scales[g][:, cols],
+                in_=e_groups[g][:, first : first + count, :, :].rearrange("p a i t -> p (a i t)"),
             )
 
-        def attend(g):
+        def attend(g, first=0, count=T, pool=psum_misc, tag="misc"):
             b, h = divmod(g, H)
-            o_ps = psum_misc.tile([P, T, HD], F32, tag="misc")
-            for ti in range(T):
+            o_ps = pool.tile([P, count, HD], F32, tag=tag)
+            for i in range(count):
+                cols = slice((first + i) * P, (first + i + 1) * P)
                 nc.tensor.matmul_mx(
-                    out=o_ps[:, ti, :],
-                    lhsT=e_codes[g][:, ti * P : (ti + 1) * P].bitcast(FP8X4),
-                    lhsT_scale=e_scales[g][:, ti * P : (ti + 1) * P],
+                    out=o_ps[:, i, :],
+                    lhsT=e_codes[g][:, cols].bitcast(FP8X4),
+                    lhsT_scale=e_scales[g][:, cols],
                     rhs=v_codes[b][:, h * HD : (h + 1) * HD].bitcast(FP8X4),
                     rhs_scale=v_scales[b][:, h * HD : (h + 1) * HD],
                     start=True,
                     stop=True,
                 )
-            o_banks[g] = o_ps
+            o_banks[g, first] = o_ps
 
         def invert_row_sums(g):
             inverse = group.tile([P, T], F32, tag="inv_sum")
             nc.vector.reciprocal(out=inverse[:], in_=row_sum[g][:])
             inv_sum[g] = inverse
 
-        def divide_and_store(g):
+        def divide_and_store(g, first=0, count=T, on_scalar=False):
             b, h = divmod(g, H)
-            o_sb = group.tile([P, T, HD], F32, tag="o")
-            nc.vector.tensor_tensor(
-                out=o_sb[:],
-                in0=o_banks[g][:],
-                in1=inv_sum[g][:].unsqueeze(2).to_broadcast([P, T, HD]),
-                op=ALU.mult,
-            )
+            o_ps = o_banks[g, first]
+            o_sb = group.tile([P, count, HD], F32, tag="o")
+            if on_scalar:
+                for i in range(count):
+                    nc.scalar.activation(
+                        out=o_sb[:, i, :], in_=o_ps[:, i, :], func=ACT.Copy,
+                        scale=inv_sum[g][:, first + i : first + i + 1],
+                    )
+            else:
+                nc.vector.tensor_tensor(
+                    out=o_sb[:],
+                    in0=o_ps[:],
+                    in1=inv_sum[g][:, first : first + count].unsqueeze(2).to_broadcast([P, count, HD]),
+                    op=ALU.mult,
+                )
             nc.sync.dma_start(
-                out=out[b].rearrange("(p t) c -> p t c", t=T)[:, :, h * HD : (h + 1) * HD], in_=o_sb[:]
+                out=out[b].rearrange("(p t) c -> p t c", t=T)[:, first : first + count, h * HD : (h + 1) * HD],
+                in_=o_sb[:],
             )
 
-        for n in range(-4, TILES + TILES_PER_BATCH):
+        for n in range(-3 - 1, TILES):
             b, j = divmod(n, TILES_PER_BATCH)
-            g1, g0 = (b - 1) * H + 1, b * H
 
-            if 0 <= n + 4 < TILES_PER_BATCH:
-                add_prior_and_mask(n + 4)
+            if b >= 0:
+                if j == 0:
+                    if b >= 2:
+                        divide_and_store(2 * b - 3)
+                elif j == 1:
+                    if b >= 1:
+                        quantise_e(2 * b - 2)
+                elif j == 2:
+                    if b < B - 1:
+                        quantise_x(b + 1, 0)
+                    if b >= 1:
+                        quantise_values(b - 1)
+                    if b >= 1:
+                        invert_row_sums(2 * b - 2)
+                elif j == 3:
+                    if b < B - 1:
+                        q_t[b + 1] = copy_heads(waiting["q"], "q_t")
+                elif j == 4:
+                    if b >= 1:
+                        divide_and_store(2 * b - 2)
+                elif j == 5:
+                    if b >= 1:
+                        quantise_e(2 * b - 1)
+                elif j == 6:
+                    if b < B - 1:
+                        quantise_x(b + 1, 1)
+                    if b >= 1:
+                        invert_row_sums(2 * b - 1)
+                elif j == 7:
+                    if b < B - 2:
+                        k_t[b + 2] = copy_heads(waiting["k"], "k_t")
+            if 0 <= n + 3 + 1 < TILES_PER_BATCH:
+                add_prior_and_mask(n + 3 + 1)
             if 0 <= n + 2 < TILES:
                 row_maximum(n + 2)
-            if j == 0:
-                if 1 <= b < B:
-                    quantise_x(b, 1)
-                if b >= 1:
-                    invert_row_sums(g1)
-            elif j == 1 and b < B - 1:
-                q_t[b + 1] = copy_heads(waiting["q"], "q_t")
-            elif j == 2 and b >= 1:
-                divide_and_store(g1 - 1)
-            elif j == 3 and b >= 1:
-                quantise_e(g1)
-            elif j == 4 and 0 <= b < B:
-                if b < B - 1:
-                    quantise_x(b + 1, 0)
-                invert_row_sums(g0)
-            elif j == 5 and 0 <= b < B - 2:
-                k_t[b + 2] = copy_heads(waiting["k"], "k_t")
-            elif j == 6 and b >= 1:
-                divide_and_store(g1)
-            elif j == 7 and 0 <= b < B:
-                quantise_e(g0)
+            if n == -2:
+                quantise_x(0, 1)
+            elif n == -1:
+                k_t[1] = copy_heads(transpose_heads(k_in[1]), "k_t")
 
-            if j in (0, 1) and b >= 1:
-                transpose_e(2 * g1 + j)
-            elif j in (4, 5) and 0 <= b < B:
-                transpose_e(2 * g0 + j - 4)
-            if j == 0 and b < B - 1:
-                waiting["q"] = transpose_heads(q_in[b + 1])
-            elif j == 4 and 0 <= b < B - 2:
-                waiting["k"] = transpose_heads(k_in[b + 2])
-            elif j in (2, 6) and 0 <= b < B - 1:
-                waiting["x", j // 4] = transpose_x(b + 1, j // 4)
+            if b >= 0:
+                if j == 0:
+                    if b >= 1:
+                        transpose_e(8 * b - 2)
+                elif j == 3:
+                    transpose_e(8 * b + 0)
+                elif j == 4:
+                    transpose_e(8 * b + 2)
+                elif j == 7:
+                    transpose_e(8 * b + 4)
+            if b >= 0:
+                if j == 0:
+                    if b < B - 1:
+                        waiting["x", 0] = transpose_x(b + 1, 0)
+                elif j == 2:
+                    if b < B - 1:
+                        waiting["q"] = transpose_heads(q_in[b + 1])
+                elif j == 4:
+                    if b < B - 1:
+                        waiting["x", 1] = transpose_x(b + 1, 1)
+                elif j == 6:
+                    if b < B - 2:
+                        waiting["k"] = transpose_heads(k_in[b + 2])
             if 0 <= n + 3 < TILES:
                 multiply_queries_and_keys(n + 3)
-            if j in (1, 5) and b >= 1:
-                attend(g1 - 1 + j // 4)
-            elif j in (3, 7) and 0 <= b < B:
-                waiting["v", j // 4] = project_values(b, j // 4)
+            if b >= 0:
+                if j == 1:
+                    waiting["v", 0] = project_values(b, 0)
+                elif j == 3:
+                    if b >= 1:
+                        attend(2 * (b - 1))
+                elif j == 5:
+                    waiting["v", 1] = project_values(b, 1)
+                elif j == 7:
+                    if b >= 1:
+                        attend(2 * (b - 1) + 1)
             if 0 <= n + 3 < TILES:
                 add_bias_to_scores(n + 3)
 
-            if j == 0 and b >= 1:
-                copy_values(b - 1, 1, waiting["v", 1])
-            elif j == 4 and 0 <= b < B:
-                copy_values(b, 0, waiting["v", 0])
-            elif j in (1, 2) and b >= 1:
-                group_e(2 * g1 + j - 1)
-            elif j in (5, 6) and 0 <= b < B:
-                group_e(2 * g0 + j - 5)
-            elif j in (3, 7) and 0 <= b < B - 1:
-                copy_x(b + 1, j // 4, waiting["x", j // 4])
+            if b >= 0:
+                if j == 0:
+                    if b >= 1:
+                        group_e(8 * b - 4)
+                elif j == 1:
+                    if b < B - 1:
+                        copy_x(b + 1, 0, waiting["x", 0])
+                elif j == 2:
+                    copy_values(b, 0, waiting["v", 0])
+                elif j == 3:
+                    if b >= 1:
+                        group_e(8 * b - 2)
+                elif j == 4:
+                    group_e(8 * b + 0)
+                elif j == 5:
+                    if b < B - 1:
+                        copy_x(b + 1, 1, waiting["x", 1])
+                elif j == 6:
+                    copy_values(b, 1, waiting["v", 1])
+                elif j == 7:
+                    group_e(8 * b + 2)
             if 0 <= n < TILES:
                 exponent(n)
-            if j == 0 and b >= 1:
-                quantise_values(b - 1)
+
+        g0, g1 = TILES // T - 2, TILES // T - 1
+        quantise_values(B - 1)
+        quantise_e(g0)
+        transpose_e(TILES - 2, 1, psum_s, "s")
+        transpose_e(TILES - 1, 1, psum_s, "s")
+        attend(g0)
+        divide_and_store(g0 - 1)
+        group_e(TILES - 4, 2, nc.vector.tensor_copy)
+        invert_row_sums(g0)
+        invert_row_sums(g1)
+        quantise_e(g1, 0, 2)
+        group_e(TILES - 2, 1)
+        group_e(TILES - 1, 1)
+        attend(g1, 0, 2, psum_s, "s")
+        quantise_e(g1, 2, 2)
+        attend(g1, 2, 2, psum_s, "s")
+        divide_and_store(g0, 0, T, True)
+        divide_and_store(g1, 0, 2)
+        divide_and_store(g1, 2, 2)

@@ -34,8 +34,10 @@ def tile_bayesianattention_pa_t_kernel(tc, x, wv, q, k, mask, shape, scale, loc,
         group = ctx.enter_context(tc.tile_pool(name="group", bufs=4))
         rows = ctx.enter_context(tc.tile_pool(name="rows", bufs=8))
         psum_s = ctx.enter_context(tc.psum_pool(name="psum_s", bufs=4))
-        psum_et = ctx.enter_context(tc.psum_pool(name="psum_et", bufs=2))
-        psum_misc = ctx.enter_context(tc.psum_pool(name="psum_misc", bufs=2))
+        psum_et = ctx.enter_context(tc.psum_pool(name="psum_et", bufs=1))
+        psum_qk = ctx.enter_context(tc.psum_pool(name="psum_qk", bufs=1))
+        psum_x = ctx.enter_context(tc.psum_pool(name="psum_x", bufs=1))
+        psum_mx = ctx.enter_context(tc.psum_pool(name="psum_mx", bufs=1))
 
         def load_parameter(param, name):
             row = const.tile([P, H], BF16, name=name)
@@ -108,9 +110,13 @@ def tile_bayesianattention_pa_t_kernel(tc, x, wv, q, k, mask, shape, scale, loc,
         for h in range(H):
             prior_h = const.tile([P, T, P + 1], F32, name="prior%d" % h)
             prior.append(prior_h)
-            nc.scalar.activation(
-                out=prior_h[:], in_=dist[:], func=ACT.Abs,
-                scale=slope[:, h : h + 1], bias=shift[:, h : h + 1],
+            z = const.tile([P, T, P + 1], F32, name="z%d" % h)
+            nc.vector.tensor_scalar(
+                out=z[:], in0=dist[:], scalar1=slope[:, h : h + 1], scalar2=shift[:, h : h + 1],
+                op0=ALU.mult, op1=ALU.add,
+            )
+            nc.vector.scalar_tensor_tensor(
+                out=prior_h[:], in0=z[:], scalar=-1.0, in1=z[:], op0=ALU.mult, op1=ALU.max
             )
         for h in range(H):
             nc.scalar.activation(out=prior[h][:], in_=prior[h][:], func=ACT.Ln, bias=EPS)
@@ -124,11 +130,11 @@ def tile_bayesianattention_pa_t_kernel(tc, x, wv, q, k, mask, shape, scale, loc,
         q_t, k_t, x_grouped, x_codes, x_scales = {}, {}, {}, {}, {}
         v_grouped, v_codes, v_scales = {}, {}, {}
 
-        def transpose_heads(src, pool=psum_misc, tag="misc"):
-            t_ps = pool.tile([P, H, T, P], BF16, tag=tag)
-            for h in range(H):
-                for t in range(T):
-                    nc.tensor.transpose(t_ps[:, h, t, :], src[:, t, h * HD : (h + 1) * HD], ident_bf[:])
+        def transpose_heads(src, h, t_ps=None):
+            if t_ps is None:
+                t_ps = psum_qk.tile([P, H, T, P], BF16, tag="qk")
+            for t in range(T):
+                nc.tensor.transpose(t_ps[:, h, t, :], src[:, t, h * HD : (h + 1) * HD], ident_bf[:])
             return t_ps
 
         def copy_heads(t_ps, tag):
@@ -136,12 +142,12 @@ def tile_bayesianattention_pa_t_kernel(tc, x, wv, q, k, mask, shape, scale, loc,
             nc.vector.tensor_copy(out=t_sb[:], in_=t_ps[:])
             return t_sb
 
-        def transpose_x(b, half, pool=psum_misc, tag="misc"):
-            x_ps = pool.tile([P, 2, 2, P], F32, tag=tag)
-            for t2 in range(2):
-                x_words = x_in[b][:, 2 * half + t2, :].bitcast(F32)
-                for u in range(2):
-                    nc.tensor.transpose(x_ps[:, t2, u, :], x_words[:, u * P : (u + 1) * P], ident_f32[:])
+        def transpose_x(b, t, x_ps=None):
+            if x_ps is None:
+                x_ps = psum_x.tile([P, 2, 2, P], F32, tag="x")
+            x_words = x_in[b][:, t, :].bitcast(F32)
+            for u in range(2):
+                nc.tensor.transpose(x_ps[:, t % 2, u, :], x_words[:, u * P : (u + 1) * P], ident_f32[:])
             return x_ps
 
         def copy_x(b, half, x_ps, on_scalar=True):
@@ -168,7 +174,7 @@ def tile_bayesianattention_pa_t_kernel(tc, x, wv, q, k, mask, shape, scale, loc,
             )
 
         def project_values(b, h):
-            v_ps = psum_misc.tile([P, T, HD], F32, tag="misc")
+            v_ps = psum_mx.tile([P, T, HD], F32, tag="mx")
             for t in range(T):
                 nc.tensor.matmul_mx(
                     out=v_ps[:, t, :],
@@ -187,25 +193,25 @@ def tile_bayesianattention_pa_t_kernel(tc, x, wv, q, k, mask, shape, scale, loc,
                 v_grouped[b] = grouped
             nc.scalar.copy(out=v_grouped[b][:, h, :, :], in_=v_ps[:].rearrange("p t d -> p d t"))
 
-        def quantise_values(b):
-            codes = batch.tile([P, E], U32, tag="v_codes", align_bytes=64)
-            scales = batch.tile([P, E], U8, tag="v_scales", align_bytes=64)
+        def quantise_values(b, h):
+            if h == 0:
+                codes = batch.tile([P, E], U32, tag="v_codes", align_bytes=64)
+                scales = batch.tile([P, E], U8, tag="v_scales", align_bytes=64)
+                v_codes[b], v_scales[b] = codes, scales
+            cols = slice(h * HD, (h + 1) * HD)
             nc.vector.quantize_mx(
-                out=codes[:].bitcast(FP8X4),
-                scales=scales[:],
-                in_=v_grouped[b][:].rearrange("p h d t -> p (h d t)"),
+                out=v_codes[b][:, cols].bitcast(FP8X4),
+                scales=v_scales[b][:, cols],
+                in_=v_grouped[b][:, h, :, :].rearrange("p d t -> p (d t)"),
             )
-            v_codes[b], v_scales[b] = codes, scales
 
         mask_t = const.tile([P, T, T, P], F32)
 
-        def transpose_mask(half):
-            mask_ps = psum_et.tile([P, 2, 2, P], F32, tag="et")
+        def transpose_mask(half, mask_ps):
             for ti2 in range(2):
                 words = mask_sb[:, 2 * half + ti2, :].bitcast(F32).rearrange("p (j u) -> p u j", u=2)
                 for u in range(2):
                     nc.tensor.transpose(mask_ps[:, ti2, u, :], words[:, u, :], ident_f32[:])
-            return mask_ps
 
         def scale_mask(half, mask_ps):
             for ti2 in range(2):
@@ -215,30 +221,40 @@ def tile_bayesianattention_pa_t_kernel(tc, x, wv, q, k, mask, shape, scale, loc,
                     scalar1=math.sqrt(HD), scalar2=0.0, op0=ALU.mult, op1=ALU.add,
                 )
 
-        q_ps = transpose_heads(q_in[0])
-        k_ps = transpose_heads(k_in[0])
+        q_ps = transpose_heads(q_in[0], 0)
+        transpose_heads(q_in[0], 1, q_ps)
+        k_ps = psum_s.tile([P, H, T, P], BF16, tag="s")
+        for h in range(H):
+            transpose_heads(k_in[0], h, k_ps)
         q_t[0] = copy_heads(q_ps, "q_t")
         k_t[0] = copy_heads(k_ps, "k_t")
-        mask_banks = [transpose_mask(0), transpose_mask(1)]
-        scale_mask(0, mask_banks[0])
-        scale_mask(1, mask_banks[1])
+        mask_low = psum_et.tile([P, 2, 2, P], F32, tag="et")
+        transpose_mask(0, mask_low)
+        mask_high = psum_mx.tile([P, 2, 2, P], F32, tag="mx")
+        transpose_mask(1, mask_high)
+        scale_mask(0, mask_low)
+        scale_mask(1, mask_high)
         x_low = transpose_x(0, 0)
-        x_high = transpose_x(0, 1)
-        copy_x(0, 0, x_low, False)
+        transpose_x(0, 1, x_low)
+        x_high = psum_s.tile([P, 2, 2, P], F32, tag="s")
+        for t in range(2, T):
+            transpose_x(0, t, x_high)
+        copy_x(0, 0, x_low)
         copy_x(0, 1, x_high)
-        quantise_x(0, 0)
+        next_k_ps = psum_et.tile([P, H, T, P], BF16, tag="et")
+        for h in range(H):
+            transpose_heads(k_in[1], h, next_k_ps)
+        waiting["k"] = next_k_ps
         wv_codes = const.tile([P, E], U32, align_bytes=64)
         wv_scales = const.tile([P, E], U8, align_bytes=64)
-        nc.vector.quantize_mx(
-            out=wv_codes[:].bitcast(FP8X4),
-            scales=wv_scales[:],
-            in_=wv_grouped[:].rearrange("p c t -> p (c t)"),
-        )
         warm_ps = psum_s.tile([P, T, P], F32, tag="s")
-        for i in range(8):
+        for i in range(6):
             nc.tensor.matmul(
-                out=warm_ps[:].rearrange("p t j -> p (t j)"), lhsT=ident_bf[:],
-                rhs=k_t[0][:, 0, :, :].rearrange("p t j -> p (t j)"), start=True, stop=True,
+                out=warm_ps[:].rearrange("p t j -> p (t j)"),
+                lhsT=ident_bf[:],
+                rhs=k_t[0][:, 0, :, :].rearrange("p t j -> p (t j)"),
+                start=True,
+                stop=True,
             )
 
         added = []
@@ -356,7 +372,7 @@ def tile_bayesianattention_pa_t_kernel(tc, x, wv, q, k, mask, shape, scale, loc,
                 in_=e_groups[g][:, first : first + count, :, :].rearrange("p a i t -> p (a i t)"),
             )
 
-        def attend(g, first=0, count=T, pool=psum_misc, tag="misc"):
+        def attend(g, first=0, count=T, pool=psum_mx, tag="mx"):
             b, h = divmod(g, H)
             o_ps = pool.tile([P, count, HD], F32, tag=tag)
             for i in range(count):
@@ -399,128 +415,147 @@ def tile_bayesianattention_pa_t_kernel(tc, x, wv, q, k, mask, shape, scale, loc,
                 in_=o_sb[:],
             )
 
-        for n in range(-3 - 1, TILES):
+        def scores(n):
+            multiply_queries_and_keys(n)
+            add_bias_to_scores(n)
+
+        add_prior_and_mask(0)
+        scores(0)
+        waiting["x", 0] = transpose_x(1, 0)
+        transpose_x(1, 1, waiting["x", 0])
+        copy_x(1, 0, waiting["x", 0])
+        add_prior_and_mask(1)
+        nc.vector.quantize_mx(
+            out=wv_codes[:].bitcast(FP8X4),
+            scales=wv_scales[:],
+            in_=wv_grouped[:].rearrange("p c t -> p (c t)"),
+        )
+        scores(1)
+        row_maximum(0)
+        add_prior_and_mask(2)
+        quantise_x(0, 0)
+        scores(2)
+        row_maximum(1)
+        add_prior_and_mask(3)
+        quantise_x(0, 1)
+        k_t[1] = copy_heads(waiting["k"], "k_t")
+
+        for n in range(TILES):
             b, j = divmod(n, TILES_PER_BATCH)
 
-            if b >= 0:
-                if j == 0:
-                    if b >= 2:
-                        divide_and_store(2 * b - 3)
-                elif j == 1:
-                    if b >= 1:
-                        quantise_e(2 * b - 2)
-                elif j == 2:
-                    if b < B - 1:
-                        quantise_x(b + 1, 0)
-                    if b >= 1:
-                        quantise_values(b - 1)
-                    if b >= 1:
-                        invert_row_sums(2 * b - 2)
-                elif j == 3:
-                    if b < B - 1:
-                        q_t[b + 1] = copy_heads(waiting["q"], "q_t")
-                elif j == 4:
-                    if b >= 1:
-                        divide_and_store(2 * b - 2)
-                elif j == 5:
-                    if b >= 1:
-                        quantise_e(2 * b - 1)
-                elif j == 6:
-                    if b < B - 1:
-                        quantise_x(b + 1, 1)
-                    if b >= 1:
-                        invert_row_sums(2 * b - 1)
-                elif j == 7:
-                    if b < B - 2:
-                        k_t[b + 2] = copy_heads(waiting["k"], "k_t")
-            if 0 <= n + 3 + 1 < TILES_PER_BATCH:
-                add_prior_and_mask(n + 3 + 1)
-            if 0 <= n + 2 < TILES:
+            if j == 0:
+                if b >= 1:
+                    divide_and_store(2 * b - 2)
+            elif j == 1:
+                if b >= 1:
+                    quantise_values(b - 1, 1)
+                if b + 1 < B:
+                    quantise_x(b + 1, 0)
+            elif j == 2:
+                if b >= 1:
+                    quantise_e(2 * b - 1)
+                if b >= 1:
+                    invert_row_sums(2 * b - 1)
+            elif j == 3:
+                if b + 1 < B:
+                    q_t[b + 1] = copy_heads(waiting["q"], "q_t")
+            elif j == 4:
+                if b >= 1:
+                    divide_and_store(2 * b - 1)
+            elif j == 5:
+                quantise_values(b, 0)
+                if b + 1 < B:
+                    quantise_x(b + 1, 1)
+            elif j == 6:
+                quantise_e(2 * b)
+                invert_row_sums(2 * b)
+            elif j == 7:
+                if b + 2 < B:
+                    k_t[b + 2] = copy_heads(waiting["k"], "k_t")
+            if n + 2 < TILES:
                 row_maximum(n + 2)
-            if n == -2:
-                quantise_x(0, 1)
-            elif n == -1:
-                k_t[1] = copy_heads(transpose_heads(k_in[1]), "k_t")
+            if n + 3 + 1 < TILES_PER_BATCH:
+                add_prior_and_mask(n + 3 + 1)
 
-            if b >= 0:
-                if j == 0:
-                    if b >= 1:
-                        transpose_e(8 * b - 2)
-                elif j == 3:
-                    transpose_e(8 * b + 0)
-                elif j == 4:
-                    transpose_e(8 * b + 2)
-                elif j == 7:
-                    transpose_e(8 * b + 4)
-            if b >= 0:
-                if j == 0:
-                    if b < B - 1:
-                        waiting["x", 0] = transpose_x(b + 1, 0)
-                elif j == 2:
-                    if b < B - 1:
-                        waiting["q"] = transpose_heads(q_in[b + 1])
-                elif j == 4:
-                    if b < B - 1:
-                        waiting["x", 1] = transpose_x(b + 1, 1)
-                elif j == 6:
-                    if b < B - 2:
-                        waiting["k"] = transpose_heads(k_in[b + 2])
-            if 0 <= n + 3 < TILES:
+            if j == 0:
+                if b >= 1:
+                    transpose_e(8 * b - 2)
+            elif j == 2:
+                transpose_e(8 * b)
+            elif j == 4:
+                transpose_e(8 * b + 2)
+            elif j == 6:
+                transpose_e(8 * b + 4)
+            if j == 0:
+                if b + 1 < B:
+                    waiting["q"] = transpose_heads(q_in[b + 1], 0)
+            elif j == 1:
+                if b + 1 < B:
+                    waiting["x", 1] = transpose_x(b + 1, 2)
+            elif j == 2:
+                if b + 1 < B:
+                    transpose_heads(q_in[b + 1], 1, waiting["q"])
+            elif j == 3:
+                if b + 1 < B:
+                    transpose_x(b + 1, 3, waiting["x", 1])
+            elif j == 4:
+                if b + 2 < B:
+                    waiting["k"] = transpose_heads(k_in[b + 2], 0)
+            elif j == 5:
+                if b + 2 < B:
+                    waiting["x", 0] = transpose_x(b + 2, 0)
+            elif j == 6:
+                if b + 2 < B:
+                    transpose_heads(k_in[b + 2], 1, waiting["k"])
+            elif j == 7:
+                if b + 2 < B:
+                    transpose_x(b + 2, 1, waiting["x", 0])
+            if n + 3 < TILES:
                 multiply_queries_and_keys(n + 3)
-            if b >= 0:
-                if j == 1:
-                    waiting["v", 0] = project_values(b, 0)
-                elif j == 3:
-                    if b >= 1:
-                        attend(2 * (b - 1))
-                elif j == 5:
-                    waiting["v", 1] = project_values(b, 1)
-                elif j == 7:
-                    if b >= 1:
-                        attend(2 * (b - 1) + 1)
-            if 0 <= n + 3 < TILES:
+            if j == 1:
+                waiting["v", 0] = project_values(b, 0)
+            elif j == 3:
+                if b >= 1:
+                    attend(2 * b - 1)
+            elif j == 5:
+                waiting["v", 1] = project_values(b, 1)
+            elif j == 7:
+                attend(2 * b)
+            if n + 3 < TILES:
                 add_bias_to_scores(n + 3)
 
-            if b >= 0:
-                if j == 0:
-                    if b >= 1:
-                        group_e(8 * b - 4)
-                elif j == 1:
-                    if b < B - 1:
-                        copy_x(b + 1, 0, waiting["x", 0])
-                elif j == 2:
-                    copy_values(b, 0, waiting["v", 0])
-                elif j == 3:
-                    if b >= 1:
-                        group_e(8 * b - 2)
-                elif j == 4:
-                    group_e(8 * b + 0)
-                elif j == 5:
-                    if b < B - 1:
-                        copy_x(b + 1, 1, waiting["x", 1])
-                elif j == 6:
-                    copy_values(b, 1, waiting["v", 1])
-                elif j == 7:
-                    group_e(8 * b + 2)
-            if 0 <= n < TILES:
-                exponent(n)
+            if j == 0:
+                if 1 <= b < B - 1:
+                    copy_x(b + 1, 0, waiting["x", 0])
+            elif j == 1:
+                if b >= 1:
+                    group_e(8 * b - 2)
+            elif j == 2:
+                copy_values(b, 0, waiting["v", 0])
+            elif j == 3:
+                group_e(8 * b)
+            elif j == 4:
+                if b + 1 < B:
+                    copy_x(b + 1, 1, waiting["x", 1])
+            elif j == 5:
+                group_e(8 * b + 2)
+            elif j == 6:
+                copy_values(b, 1, waiting["v", 1])
+            elif j == 7:
+                group_e(8 * b + 4)
+            exponent(n)
 
-        g0, g1 = TILES // T - 2, TILES // T - 1
-        quantise_values(B - 1)
-        quantise_e(g0)
+        g = TILES // T - 1
         transpose_e(TILES - 2, 1, psum_s, "s")
         transpose_e(TILES - 1, 1, psum_s, "s")
-        attend(g0)
-        divide_and_store(g0 - 1)
-        group_e(TILES - 4, 2, nc.vector.tensor_copy)
-        invert_row_sums(g0)
-        invert_row_sums(g1)
-        quantise_e(g1, 0, 2)
+        divide_and_store(g - 1)
+        quantise_e(g, 0, 2)
+        quantise_values(B - 1, 1)
+        invert_row_sums(g)
         group_e(TILES - 2, 1)
         group_e(TILES - 1, 1)
-        attend(g1, 0, 2, psum_s, "s")
-        quantise_e(g1, 2, 2)
-        attend(g1, 2, 2, psum_s, "s")
-        divide_and_store(g0, 0, T, True)
-        divide_and_store(g1, 0, 2)
-        divide_and_store(g1, 2, 2)
+        attend(g, 0, 2, psum_s, "s")
+        quantise_e(g, 2, 2)
+        attend(g, 2, 2, psum_s, "s")
+        divide_and_store(g, 0, 2, True)
+        divide_and_store(g, 2, 2)

@@ -248,7 +248,7 @@ def tile_bayesianattention_pa_t_kernel(tc, x, wv, q, k, mask, shape, scale, loc,
         wv_codes = const.tile([P, E], U32, align_bytes=64)
         wv_scales = const.tile([P, E], U8, align_bytes=64)
         warm_ps = psum_s.tile([P, T, P], F32, tag="s")
-        for i in range(6):
+        for i in range(2):
             nc.tensor.matmul(
                 out=warm_ps[:].rearrange("p t j -> p (t j)"),
                 lhsT=ident_bf[:],
@@ -285,6 +285,14 @@ def tile_bayesianattention_pa_t_kernel(tc, x, wv, q, k, mask, shape, scale, loc,
             g, ti = divmod(n, T)
             b, h = divmod(g, H)
             s_ps = psum_s.tile([P, T, P], F32, tag="s")
+            if 1 <= n < TILES_PER_BATCH + 1:
+                nc.tensor.matmul(
+                    out=s_ps[:, :T, :].rearrange("p t j -> p (t j)"),
+                    lhsT=q_t[b][:, h, ti, :],
+                    rhs=k_t[b][:, h, :T, :].rearrange("p t j -> p (t j)"),
+                    start=True,
+                    stop=True,
+                )
             nc.tensor.matmul(
                 out=s_ps[:].rearrange("p t j -> p (t j)"),
                 lhsT=q_t[b][:, h, ti, :],

@@ -33,11 +33,11 @@ def tile_bayesianattention_pa_t_kernel(tc, x, wv, q, k, mask, shape, scale, loc,
         batch = ctx.enter_context(tc.tile_pool(name="batch", bufs=3))
         group = ctx.enter_context(tc.tile_pool(name="group", bufs=4))
         rows = ctx.enter_context(tc.tile_pool(name="rows", bufs=8))
-        psum_s = ctx.enter_context(tc.psum_pool(name="psum_s", bufs=4))
+        psum_s = ctx.enter_context(tc.psum_pool(name="psum_s", bufs=3))
         psum_et = ctx.enter_context(tc.psum_pool(name="psum_et", bufs=1))
         psum_qk = ctx.enter_context(tc.psum_pool(name="psum_qk", bufs=1))
         psum_x = ctx.enter_context(tc.psum_pool(name="psum_x", bufs=1))
-        psum_mx = ctx.enter_context(tc.psum_pool(name="psum_mx", bufs=1))
+        psum_mx = ctx.enter_context(tc.psum_pool(name="psum_mx", bufs=2))
 
         def load_parameter(param, name):
             row = const.tile([P, H], BF16, name=name)
@@ -88,10 +88,6 @@ def tile_bayesianattention_pa_t_kernel(tc, x, wv, q, k, mask, shape, scale, loc,
         ident_f32 = const.tile([P, P], F32)
         make_identity(nc, ident_f32[:])
         wv_grouped = const.tile([P, E, T], BF16, align_bytes=64)
-        nc.gpsimd.tensor_scalar(
-            out=wv_grouped[:], in0=wv_sb[:].rearrange("p t c -> p c t"),
-            scalar1=1.0, scalar2=0.0, op0=ALU.mult, op1=ALU.add,
-        )
 
         slope = const.tile([P, H], F32)
         nc.scalar.activation(out=slope[:], in_=scale_bf[:], func=ACT.Exp)
@@ -111,7 +107,8 @@ def tile_bayesianattention_pa_t_kernel(tc, x, wv, q, k, mask, shape, scale, loc,
             prior_h = const.tile([P, T, P + 1], F32, name="prior%d" % h)
             prior.append(prior_h)
             z = const.tile([P, T, P + 1], F32, name="z%d" % h)
-            nc.vector.tensor_scalar(
+            engine = nc.vector if h == 0 else nc.gpsimd
+            engine.tensor_scalar(
                 out=z[:], in0=dist[:], scalar1=slope[:, h : h + 1], scalar2=shift[:, h : h + 1],
                 op0=ALU.mult, op1=ALU.add,
             )
@@ -125,6 +122,11 @@ def tile_bayesianattention_pa_t_kernel(tc, x, wv, q, k, mask, shape, scale, loc,
                 out=prior[h][:], in_=prior[h][:], func=ACT.Exp,
                 scale=power[:, h : h + 1], bias=0.5 * math.log(HD),
             )
+
+        nc.gpsimd.tensor_scalar(
+            out=wv_grouped[:], in0=wv_sb[:].rearrange("p t c -> p c t"),
+            scalar1=1.0, scalar2=0.0, op0=ALU.mult, op1=ALU.add,
+        )
 
         waiting = {}
         q_t, k_t, x_grouped, x_codes, x_scales = {}, {}, {}, {}, {}
@@ -161,17 +163,15 @@ def tile_bayesianattention_pa_t_kernel(tc, x, wv, q, k, mask, shape, scale, loc,
             else:
                 nc.vector.tensor_copy(out=dst, in_=src)
 
-        def quantise_x(b, half):
-            if half == 0:
-                codes = batch.tile([P, T * P], U32, tag="x_codes", align_bytes=64)
-                scales = batch.tile([P, T * P], U8, tag="x_scales", align_bytes=64)
-                x_codes[b], x_scales[b] = codes, scales
-            cols = slice(half * 2 * P, (half + 1) * 2 * P)
+        def quantise_x(b):
+            codes = batch.tile([P, T * P], U32, tag="x_codes", align_bytes=64)
+            scales = batch.tile([P, T * P], U8, tag="x_scales", align_bytes=64)
             nc.vector.quantize_mx(
-                out=x_codes[b][:, cols].bitcast(FP8X4),
-                scales=x_scales[b][:, cols],
-                in_=x_grouped[b][:, 2 * half : 2 * half + 2, :, :].rearrange("p t r w -> p (t r w)"),
+                out=codes[:].bitcast(FP8X4),
+                scales=scales[:],
+                in_=x_grouped[b][:].rearrange("p t r w -> p (t r w)"),
             )
+            x_codes[b], x_scales[b] = codes, scales
 
         def project_values(b, h):
             v_ps = psum_mx.tile([P, T, HD], F32, tag="mx")
@@ -262,7 +262,7 @@ def tile_bayesianattention_pa_t_kernel(tc, x, wv, q, k, mask, shape, scale, loc,
             added_h = const.tile([P, T, T, P], F32, name="added%d" % h)
             added.append(added_h)
         s_banks, e_rows, e_banks, e_groups = {}, {}, {}, {}
-        row_max, exp_bias, row_sum, inv_sum, e_codes, e_scales, o_banks = {}, {}, {}, {}, {}, {}, {}
+        s_rows, exp_bias, row_sum, inv_sum, e_codes, e_scales, o_banks = {}, {}, {}, {}, {}, {}, {}
 
         def add_prior_and_mask(n):
             h, ti = divmod(n, T)
@@ -318,21 +318,19 @@ def tile_bayesianattention_pa_t_kernel(tc, x, wv, q, k, mask, shape, scale, loc,
         def row_maximum(n):
             g, ti = divmod(n, T)
             if ti == 0:
-                maxima = group.tile([P, T], F32, tag="row_max")
                 biases = group.tile([P, T], F32, tag="exp_bias")
-                row_max[g], exp_bias[g] = maxima, biases
-            nc.vector.reduce_max(
-                out=row_max[g][:, ti : ti + 1], in_=s_banks[n][:].rearrange("p t j -> p (t j)"), axis=AXIS.X
-            )
-
-            nc.gpsimd.tensor_scalar(
-                out=exp_bias[g][:, ti : ti + 1],
-                in0=row_max[g][:, ti : ti + 1],
+                exp_bias[g] = biases
+            s_sb = rows.tile([P, 2, P, 2], F32, tag="s_sb", bufs=4)
+            nc.vector.tensor_scalar(
+                out=s_sb[:],
+                in0=s_banks[n][:].rearrange("p (u w) j -> p u j w", u=2),
                 scalar1=-1.0 / math.sqrt(HD),
-                scalar2=0.0,
+                scalar2=None,
                 op0=ALU.mult,
-                op1=ALU.add,
+                op1=ALU.min,
+                accum_out=exp_bias[g][:, ti : ti + 1],
             )
+            s_rows[n] = s_sb
 
         def exponent(n):
             g, ti = divmod(n, T)
@@ -342,9 +340,9 @@ def tile_bayesianattention_pa_t_kernel(tc, x, wv, q, k, mask, shape, scale, loc,
             e_sb = rows.tile([P, 2, P, 2], BF16, tag="e")
             nc.scalar.activation(
                 out=e_sb[:],
-                in_=s_banks[n][:].rearrange("p (u w) j -> p u j w", u=2),
+                in_=s_rows[n][:],
                 func=ACT.Exp,
-                scale=1.0 / math.sqrt(HD),
+                scale=-1.0,
                 bias=exp_bias[g][:, ti : ti + 1],
                 accum_out=row_sum[g][:, ti : ti + 1],
             )
@@ -441,11 +439,10 @@ def tile_bayesianattention_pa_t_kernel(tc, x, wv, q, k, mask, shape, scale, loc,
         scores(1)
         row_maximum(0)
         add_prior_and_mask(2)
-        quantise_x(0, 0)
         scores(2)
         row_maximum(1)
         add_prior_and_mask(3)
-        quantise_x(0, 1)
+        quantise_x(0)
         k_t[1] = copy_heads(waiting["k"], "k_t")
 
         for n in range(TILES):
@@ -457,8 +454,6 @@ def tile_bayesianattention_pa_t_kernel(tc, x, wv, q, k, mask, shape, scale, loc,
             elif j == 1:
                 if b >= 1:
                     quantise_values(b - 1, 1)
-                if b + 1 < B:
-                    quantise_x(b + 1, 0)
             elif j == 2:
                 if b >= 1:
                     quantise_e(2 * b - 1)
@@ -473,7 +468,7 @@ def tile_bayesianattention_pa_t_kernel(tc, x, wv, q, k, mask, shape, scale, loc,
             elif j == 5:
                 quantise_values(b, 0)
                 if b + 1 < B:
-                    quantise_x(b + 1, 1)
+                    quantise_x(b + 1)
             elif j == 6:
                 quantise_e(2 * b)
                 invert_row_sums(2 * b)
@@ -532,6 +527,7 @@ def tile_bayesianattention_pa_t_kernel(tc, x, wv, q, k, mask, shape, scale, loc,
             if n + 3 < TILES:
                 add_bias_to_scores(n + 3)
 
+            exponent(n)
             if j == 0:
                 if 1 <= b < B - 1:
                     copy_x(b + 1, 0, waiting["x", 0])
@@ -549,21 +545,22 @@ def tile_bayesianattention_pa_t_kernel(tc, x, wv, q, k, mask, shape, scale, loc,
                 group_e(8 * b + 2)
             elif j == 6:
                 copy_values(b, 1, waiting["v", 1])
-            elif j == 7:
+            elif j == 7 and b < B - 1:
                 group_e(8 * b + 4)
-            exponent(n)
 
         g = TILES // T - 1
         transpose_e(TILES - 2, 1, psum_s, "s")
         transpose_e(TILES - 1, 1, psum_s, "s")
+        quantise_values(B - 1, 1)
+        group_e(TILES - 4, 2, nc.vector.tensor_copy)
         divide_and_store(g - 1)
         quantise_e(g, 0, 2)
-        quantise_values(B - 1, 1)
+        group_e(TILES - 2, 1, nc.vector.tensor_copy)
         invert_row_sums(g)
-        group_e(TILES - 2, 1)
+        quantise_e(g, 2, 1)
         group_e(TILES - 1, 1)
-        attend(g, 0, 2, psum_s, "s")
-        quantise_e(g, 2, 2)
-        attend(g, 2, 2, psum_s, "s")
-        divide_and_store(g, 0, 2, True)
-        divide_and_store(g, 2, 2)
+        attend(g, 0, 3, psum_s, "s")
+        quantise_e(g, 3, 1)
+        attend(g, 3, 1, psum_s, "s")
+        divide_and_store(g, 0, 3)
+        divide_and_store(g, 3, 1, True)

@@ -241,10 +241,6 @@ def tile_bayesianattention_pa_t_kernel(tc, x, wv, q, k, mask, shape, scale, loc,
             transpose_x(0, t, x_high)
         copy_x(0, 0, x_low)
         copy_x(0, 1, x_high)
-        next_k_ps = psum_et.tile([P, H, T, P], BF16, tag="et")
-        for h in range(H):
-            transpose_heads(k_in[1], h, next_k_ps)
-        waiting["k"] = next_k_ps
         wv_codes = const.tile([P, E], U32, align_bytes=64)
         wv_scales = const.tile([P, E], U8, align_bytes=64)
         warm_ps = psum_s.tile([P, T, P], F32, tag="s")
@@ -285,7 +281,7 @@ def tile_bayesianattention_pa_t_kernel(tc, x, wv, q, k, mask, shape, scale, loc,
             g, ti = divmod(n, T)
             b, h = divmod(g, H)
             s_ps = psum_s.tile([P, T, P], F32, tag="s")
-            if 1 <= n < TILES_PER_BATCH + 1:
+            if 1 <= n <= 6:
                 nc.tensor.matmul(
                     out=s_ps[:, :T, :].rearrange("p t j -> p (t j)"),
                     lhsT=q_t[b][:, h, ti, :],
@@ -437,6 +433,10 @@ def tile_bayesianattention_pa_t_kernel(tc, x, wv, q, k, mask, shape, scale, loc,
             in_=wv_grouped[:].rearrange("p c t -> p (c t)"),
         )
         scores(1)
+        next_k_ps = psum_et.tile([P, H, T, P], BF16, tag="et")
+        for h in range(H):
+            transpose_heads(k_in[1], h, next_k_ps)
+        waiting["k"] = next_k_ps
         row_maximum(0)
         add_prior_and_mask(2)
         scores(2)

import math
from contextlib import ExitStack

import concourse.mybir as mybir
from concourse.masks import make_identity

F32 = mybir.dt.float32
BF16 = mybir.dt.bfloat16
U32 = mybir.dt.uint32
U8 = mybir.dt.uint8
FP8X4 = mybir.dt.float8_e4m3fn_x4
ACT = mybir.ActivationFunctionType
ALU = mybir.AluOpType
AXIS = mybir.AxisListType

B, S, D, H, HD = 8, 512, 512, 2, 128
E = H * HD
EPS = 1e-5
P = 128
T = 4
TILES = B * H * T
TILES_PER_BATCH = H * T

FLOPS = 2 * B * S * D * E + 2 * 2 * B * H * S * S * HD


def tile_bayesianattention_pa_t_kernel(tc, x, wv, q, k, mask, shape, scale, loc, out):
    nc = tc.nc
    with ExitStack() as ctx:
        ctx.enter_context(tc.manual_schedule())
        const = ctx.enter_context(tc.tile_pool(name="const", bufs=1))
        inputs = ctx.enter_context(tc.tile_pool(name="inputs", bufs=B))
        batch = ctx.enter_context(tc.tile_pool(name="batch", bufs=3))
        group = ctx.enter_context(tc.tile_pool(name="group", bufs=4))
        rows = ctx.enter_context(tc.tile_pool(name="rows", bufs=8))
        psum_s = ctx.enter_context(tc.psum_pool(name="psum_s", bufs=3))
        psum_et = ctx.enter_context(tc.psum_pool(name="psum_et", bufs=1))
        psum_qk = ctx.enter_context(tc.psum_pool(name="psum_qk", bufs=1))
        psum_x = ctx.enter_context(tc.psum_pool(name="psum_x", bufs=1))
        psum_mx = ctx.enter_context(tc.psum_pool(name="psum_mx", bufs=2))

        def load_parameter(param, name):
            row = const.tile([P, H], BF16, name=name)
            nc.sync.dma_start(
                out=row[:], in_=param.rearrange("a h b c -> (a h b c)").partition_broadcast(P)
            )
            return row

        scale_bf = load_parameter(scale, "scale_bf")
        loc_bf = load_parameter(loc, "loc_bf")
        shape_bf = load_parameter(shape, "shape_bf")

        q_in, k_in, x_in = {}, {}, {}

        def load_queries_and_keys(b):
            q_sb = inputs.tile([P, T, E], BF16, tag="q")
            nc.sync.dma_start(out=q_sb[:], in_=q[b].rearrange("(p t) h d -> p t (h d)", t=T))
            k_sb = inputs.tile([P, T, E], BF16, tag="k")
            nc.sync.dma_start(out=k_sb[:], in_=k[b].rearrange("(p t) h d -> p t (h d)", t=T))
            q_in[b], k_in[b] = q_sb, k_sb

        def load_x(b):
            x_sb = inputs.tile([P, T, D], BF16, tag="x")
            nc.sync.dma_start(out=x_sb[:], in_=x[b].rearrange("(p t) f -> p t f", t=T))
            x_in[b] = x_sb

        load_queries_and_keys(0)
        mask_sb = const.tile([P, T, S], BF16)
        nc.sync.dma_start(out=mask_sb[:], in_=mask[0, 0].rearrange("(p t) j -> p t j", t=T))
        wv_sb = const.tile([P, T, E], BF16)
        for u in range(2):
            nc.sync.dma_start(
                out=wv_sb[:, 2 * u : 2 * u + 2, :],
                in_=wv[2 * P * u : 2 * P * (u + 1), :].rearrange("(p e) c -> p e c", e=2),
            )
        load_x(0)
        for b in range(1, B):
            load_queries_and_keys(b)
            load_x(b)

        ident_bf = const.tile([P, P], BF16)
        make_identity(nc, ident_bf[:])
        dist = const.tile([P, T, P + 1], F32)
        nc.gpsimd.iota(
            dist[:], pattern=[[1, T], [-T, P + 1]], base=1, channel_multiplier=T,
            allow_small_or_imprecise_dtypes=True,
        )
        ident_f32 = const.tile([P, P], F32)
        make_identity(nc, ident_f32[:])
        wv_grouped = const.tile([P, E, T], BF16, align_bytes=64)

        slope = const.tile([P, H], F32)
        nc.scalar.activation(out=slope[:], in_=scale_bf[:], func=ACT.Exp)
        exp_loc = const.tile([P, H], F32)
        nc.scalar.activation(out=exp_loc[:], in_=loc_bf[:], func=ACT.Exp)
        exp_neg_loc = const.tile([P, H], F32)
        nc.scalar.activation(out=exp_neg_loc[:], in_=loc_bf[:], func=ACT.Exp, scale=-1.0)
        ln_table = const.tile([P, 1], F32)
        nc.scalar.activation(out=ln_table[:], in_=slope[:, :1], func=ACT.Ln)
        shift = const.tile([P, H], F32)
        nc.vector.tensor_sub(out=shift[:], in0=exp_neg_loc[:], in1=exp_loc[:])
        nc.vector.tensor_mul(out=shift[:], in0=shift[:], in1=slope[:])
        power = const.tile([P, H], F32)
        nc.vector.tensor_copy(out=power[:], in_=shape_bf[:])
        prior = []
        for h in range(H):
            prior_h = const.tile([P, T, P + 1], F32, name="prior%d" % h)
            prior.append(prior_h)
            z = const.tile([P, T, P + 1], F32, name="z%d" % h)
            engine = nc.vector if h == 0 else nc.gpsimd
            engine.tensor_scalar(
                out=z[:], in0=dist[:], scalar1=slope[:, h : h + 1], scalar2=shift[:, h : h + 1],
                op0=ALU.mult, op1=ALU.add,
            )
            nc.vector.scalar_tensor_tensor(
                out=prior_h[:], in0=z[:], scalar=-1.0, in1=z[:], op0=ALU.mult, op1=ALU.max
            )
        for h in range(H):
            nc.scalar.activation(out=prior[h][:], in_=prior[h][:], func=ACT.Ln, bias=EPS)
        for h in range(H):
            nc.scalar.activation(
                out=prior[h][:], in_=prior[h][:], func=ACT.Exp,
                scale=power[:, h : h + 1], bias=0.5 * math.log(HD),
            )

        nc.gpsimd.tensor_scalar(
            out=wv_grouped[:], in0=wv_sb[:].rearrange("p t c -> p c t"),
            scalar1=1.0, scalar2=0.0, op0=ALU.mult, op1=ALU.add,
        )

        waiting = {}
        q_t, k_t, x_grouped, x_codes, x_scales = {}, {}, {}, {}, {}
        v_grouped, v_codes, v_scales = {}, {}, {}

        def transpose_heads(src, h, t_ps=None):
            if t_ps is None:
                t_ps = psum_qk.tile([P, H, T, P], BF16, tag="qk")
            for t in range(T):
                nc.tensor.transpose(t_ps[:, h, t, :], src[:, t, h * HD : (h + 1) * HD], ident_bf[:])
            return t_ps

        def copy_heads(t_ps, tag):
            t_sb = batch.tile([P, H, T, P], BF16, tag=tag)
            nc.vector.tensor_copy(out=t_sb[:], in_=t_ps[:])
            return t_sb

        def transpose_x(b, t, x_ps=None):
            if x_ps is None:
                x_ps = psum_x.tile([P, 2, 2, P], F32, tag="x")
            x_words = x_in[b][:, t, :].bitcast(F32)
            for u in range(2):
                nc.tensor.transpose(x_ps[:, t % 2, u, :], x_words[:, u * P : (u + 1) * P], ident_f32[:])
            return x_ps

        def copy_x(b, half, x_ps, on_scalar=True):
            if half == 0:
                grouped = batch.tile([P, T, P, T], BF16, tag="x_grouped", align_bytes=64)
                x_grouped[b] = grouped
            dst = x_grouped[b][:, 2 * half : 2 * half + 2, :, :].bitcast(F32)
            src = x_ps[:].rearrange("p t u r -> p t r u")
            if on_scalar:
                nc.scalar.copy(out=dst, in_=src)
            else:
                nc.vector.tensor_copy(out=dst, in_=src)

        def quantise_x(b):
            codes = batch.tile([P, T * P], U32, tag="x_codes", align_bytes=64)
            scales = batch.tile([P, T * P], U8, tag="x_scales", align_bytes=64)
            nc.vector.quantize_mx(
                out=codes[:].bitcast(FP8X4),
                scales=scales[:],
                in_=x_grouped[b][:].rearrange("p t r w -> p (t r w)"),
            )
            x_codes[b], x_scales[b] = codes, scales

        def project_values(b, h):
            v_ps = psum_mx.tile([P, T, HD], F32, tag="mx")
            for t in range(T):
                nc.tensor.matmul_mx(
                    out=v_ps[:, t, :],
                    lhsT=x_codes[b][:, t * P : (t + 1) * P].bitcast(FP8X4),
                    lhsT_scale=x_scales[b][:, t * P : (t + 1) * P],
                    rhs=wv_codes[:, h * HD : (h + 1) * HD].bitcast(FP8X4),
                    rhs_scale=wv_scales[:, h * HD : (h + 1) * HD],
                    start=True,
                    stop=True,
                )
            return v_ps

        def copy_values(b, h, v_ps):
            if h == 0:
                grouped = batch.tile([P, H, HD, T], BF16, tag="v_grouped", align_bytes=64)
                v_grouped[b] = grouped
            nc.scalar.copy(out=v_grouped[b][:, h, :, :], in_=v_ps[:].rearrange("p t d -> p d t"))

        def quantise_values(b, h):
            if h == 0:
                codes = batch.tile([P, E], U32, tag="v_codes", align_bytes=64)
                scales = batch.tile([P, E], U8, tag="v_scales", align_bytes=64)
                v_codes[b], v_scales[b] = codes, scales
            cols = slice(h * HD, (h + 1) * HD)
            nc.vector.quantize_mx(
                out=v_codes[b][:, cols].bitcast(FP8X4),
                scales=v_scales[b][:, cols],
                in_=v_grouped[b][:, h, :, :].rearrange("p d t -> p (d t)"),
            )

        mask_t = const.tile([P, T, T, P], F32)

        def transpose_mask(half, mask_ps):
            for ti2 in range(2):
                words = mask_sb[:, 2 * half + ti2, :].bitcast(F32).rearrange("p (j u) -> p u j", u=2)
                for u in range(2):
                    nc.tensor.transpose(mask_ps[:, ti2, u, :], words[:, u, :], ident_f32[:])

        def scale_mask(half, mask_ps):
            for ti2 in range(2):
                nc.vector.tensor_scalar(
                    out=mask_t[:, 2 * half + ti2, :, :].rearrange("p (u w) i -> p u w i", u=2),
                    in0=mask_ps[:, ti2, :, :].bitcast(BF16).rearrange("p u (i w) -> p u w i", w=2),
                    scalar1=math.sqrt(HD), scalar2=0.0, op0=ALU.mult, op1=ALU.add,
                )

        q_ps = transpose_heads(q_in[0], 0)
        transpose_heads(q_in[0], 1, q_ps)
        k_ps = psum_s.tile([P, H, T, P], BF16, tag="s")
        for h in range(H):
            transpose_heads(k_in[0], h, k_ps)
        q_t[0] = copy_heads(q_ps, "q_t")
        k_t[0] = copy_heads(k_ps, "k_t")
        mask_low = psum_et.tile([P, 2, 2, P], F32, tag="et")
        transpose_mask(0, mask_low)
        mask_high = psum_mx.tile([P, 2, 2, P], F32, tag="mx")
        transpose_mask(1, mask_high)
        scale_mask(0, mask_low)
        scale_mask(1, mask_high)
        x_low = transpose_x(0, 0)
        transpose_x(0, 1, x_low)
        x_high = psum_s.tile([P, 2, 2, P], F32, tag="s")
        for t in range(2, T):
            transpose_x(0, t, x_high)
        copy_x(0, 0, x_low)
        copy_x(0, 1, x_high)
        wv_codes = const.tile([P, E], U32, align_bytes=64)
        wv_scales = const.tile([P, E], U8, align_bytes=64)
        warm_ps = psum_s.tile([P, T, P], F32, tag="s")
        for i in range(2):
            nc.tensor.matmul(
                out=warm_ps[:].rearrange("p t j -> p (t j)"),
                lhsT=ident_bf[:],
                rhs=k_t[0][:, 0, :, :].rearrange("p t j -> p (t j)"),
                start=True,
                stop=True,
            )

        added = []
        for h in range(H):
            added_h = const.tile([P, T, T, P], F32, name="added%d" % h)
            added.append(added_h)
        s_banks, e_rows, e_banks, e_groups = {}, {}, {}, {}
        s_rows, exp_bias, row_sum, inv_sum, e_codes, e_scales, o_banks = {}, {}, {}, {}, {}, {}, {}

        def add_prior_and_mask(n):
            h, ti = divmod(n, T)
            engine = nc.vector
            engine.tensor_tensor(
                out=added[h][:, ti, : ti + 1, :],
                in0=mask_t[:, ti, : ti + 1, :],
                in1=prior[h][:, T - 1 - ti :, 1:],
                op=ALU.subtract,
            )
            if ti < T - 1:
                engine.tensor_tensor(
                    out=added[h][:, ti, ti + 1 :, :],
                    in0=mask_t[:, ti, ti + 1 :, :],
                    in1=prior[h][:, : T - 1 - ti, :P],
                    op=ALU.subtract,
                )

        def multiply_queries_and_keys(n):
            g, ti = divmod(n, T)
            b, h = divmod(g, H)
            s_ps = psum_s.tile([P, T, P], F32, tag="s")
            if 1 <= n <= 6:
                nc.tensor.matmul(
                    out=s_ps[:, :T, :].rearrange("p t j -> p (t j)"),
                    lhsT=q_t[b][:, h, ti, :],
                    rhs=k_t[b][:, h, :T, :].rearrange("p t j -> p (t j)"),
                    start=True,
                    stop=True,
                )
            nc.tensor.matmul(
                out=s_ps[:].rearrange("p t j -> p (t j)"),
                lhsT=q_t[b][:, h, ti, :],
                rhs=k_t[b][:, h, :, :].rearrange("p t j -> p (t j)"),
                start=True,
                stop=False,
            )
            s_banks[n] = s_ps

        def add_bias_to_scores(n):
            g, ti = divmod(n, T)
            h = g % H
            for t in range(T):
                nc.tensor.matmul(
                    out=s_banks[n][:, t, :],
                    lhsT=added[h][:, ti, t, :],
                    rhs=ident_f32[:],
                    is_transpose=True,
                    start=False,
                    stop=(t == T - 1),
                )

        def row_maximum(n):
            g, ti = divmod(n, T)
            if ti == 0:
                biases = group.tile([P, T], F32, tag="exp_bias")
                exp_bias[g] = biases
            s_sb = rows.tile([P, 2, P, 2], F32, tag="s_sb", bufs=4)
            nc.vector.tensor_scalar(
                out=s_sb[:],
                in0=s_banks[n][:].rearrange("p (u w) j -> p u j w", u=2),
                scalar1=-1.0 / math.sqrt(HD),
                scalar2=None,
                op0=ALU.mult,
                op1=ALU.min,
                accum_out=exp_bias[g][:, ti : ti + 1],
            )
            s_rows[n] = s_sb

        def exponent(n):
            g, ti = divmod(n, T)
            if ti == 0:
                sums = group.tile([P, T], F32, tag="row_sum")
                row_sum[g] = sums
            e_sb = rows.tile([P, 2, P, 2], BF16, tag="e")
            nc.scalar.activation(
                out=e_sb[:],
                in_=s_rows[n][:],
                func=ACT.Exp,
                scale=-1.0,
                bias=exp_bias[g][:, ti : ti + 1],
                accum_out=row_sum[g][:, ti : ti + 1],
            )
            e_rows[n] = e_sb

        def transpose_e(first, count=2, pool=psum_et, tag="et"):
            e_ps = pool.tile([P, count, 2, P], F32, tag=tag)
            for i in range(count):
                e_words = e_rows[first + i][:].rearrange("p u j w -> p (u j w)").bitcast(F32)
                for u in range(2):
                    nc.tensor.transpose(e_ps[:, i, u, :], e_words[:, u * P : (u + 1) * P], ident_f32[:])
            e_banks[first] = e_ps

        def group_e(first, count=2, copy=nc.scalar.copy):
            g, ti = divmod(first, T)
            if ti == 0:
                grouped = group.tile([P, T, P, T], BF16, tag="e_grouped", align_bytes=64)
                e_groups[g] = grouped
            copy(
                out=e_groups[g][:, ti : ti + count, :, :].bitcast(F32),
                in_=e_banks[first][:].rearrange("p a u i -> p a i u"),
            )

        def quantise_e(g, first=0, count=T):
            if first == 0:
                codes = group.tile([P, T * P], U32, tag="e_codes", align_bytes=64)
                scales = group.tile([P, T * P], U8, tag="e_scales", align_bytes=64)
                e_codes[g], e_scales[g] = codes, scales
            cols = slice(first * P, (first + count) * P)
            nc.vector.quantize_mx(
                out=e_codes[g][:, cols].bitcast(FP8X4),
                scales=e_scales[g][:, cols],
                in_=e_groups[g][:, first : first + count, :, :].rearrange("p a i t -> p (a i t)"),
            )

        def attend(g, first=0, count=T, pool=psum_mx, tag="mx"):
            b, h = divmod(g, H)
            o_ps = pool.tile([P, count, HD], F32, tag=tag)
            for i in range(count):
                cols = slice((first + i) * P, (first + i + 1) * P)
                nc.tensor.matmul_mx(
                    out=o_ps[:, i, :],
                    lhsT=e_codes[g][:, cols].bitcast(FP8X4),
                    lhsT_scale=e_scales[g][:, cols],
                    rhs=v_codes[b][:, h * HD : (h + 1) * HD].bitcast(FP8X4),
                    rhs_scale=v_scales[b][:, h * HD : (h + 1) * HD],
                    start=True,
                    stop=True,
                )
            o_banks[g, first] = o_ps

        def invert_row_sums(g):
            inverse = group.tile([P, T], F32, tag="inv_sum")
            nc.vector.reciprocal(out=inverse[:], in_=row_sum[g][:])
            inv_sum[g] = inverse

        def divide_and_store(g, first=0, count=T, on_scalar=False):
            b, h = divmod(g, H)
            o_ps = o_banks[g, first]
            o_sb = group.tile([P, count, HD], F32, tag="o")
            if on_scalar:
                for i in range(count):
                    nc.scalar.activation(
                        out=o_sb[:, i, :], in_=o_ps[:, i, :], func=ACT.Copy,
                        scale=inv_sum[g][:, first + i : first + i + 1],
                    )
            else:
                nc.vector.tensor_tensor(
                    out=o_sb[:],
                    in0=o_ps[:],
                    in1=inv_sum[g][:, first : first + count].unsqueeze(2).to_broadcast([P, count, HD]),
                    op=ALU.mult,
                )
            nc.sync.dma_start(
                out=out[b].rearrange("(p t) c -> p t c", t=T)[:, first : first + count, h * HD : (h + 1) * HD],
                in_=o_sb[:],
            )

        def scores(n):
            multiply_queries_and_keys(n)
            add_bias_to_scores(n)

        add_prior_and_mask(0)
        scores(0)
        waiting["x", 0] = transpose_x(1, 0)
        transpose_x(1, 1, waiting["x", 0])
        copy_x(1, 0, waiting["x", 0])
        add_prior_and_mask(1)
        nc.vector.quantize_mx(
            out=wv_codes[:].bitcast(FP8X4),
            scales=wv_scales[:],
            in_=wv_grouped[:].rearrange("p c t -> p (c t)"),
        )
        scores(1)
        next_k_ps = psum_et.tile([P, H, T, P], BF16, tag="et")
        for h in range(H):
            transpose_heads(k_in[1], h, next_k_ps)
        waiting["k"] = next_k_ps
        row_maximum(0)
        add_prior_and_mask(2)
        scores(2)
        row_maximum(1)
        add_prior_and_mask(3)
        quantise_x(0)
        k_t[1] = copy_heads(waiting["k"], "k_t")

        for n in range(TILES):
            b, j = divmod(n, TILES_PER_BATCH)

            if j == 0:
                if b >= 1:
                    divide_and_store(2 * b - 2)
            elif j == 1:
                if b >= 1:
                    quantise_values(b - 1, 1)
            elif j == 2:
                if b >= 1:
                    quantise_e(2 * b - 1)
                if b >= 1:
                    invert_row_sums(2 * b - 1)
            elif j == 3:
                if b + 1 < B:
                    q_t[b + 1] = copy_heads(waiting["q"], "q_t")
            elif j == 4:
                if b >= 1:
                    divide_and_store(2 * b - 1)
            elif j == 5:
                quantise_values(b, 0)
                if b + 1 < B:
                    quantise_x(b + 1)
            elif j == 6:
                quantise_e(2 * b)
                invert_row_sums(2 * b)
            elif j == 7:
                if b + 2 < B:
                    k_t[b + 2] = copy_heads(waiting["k"], "k_t")
            if n + 2 < TILES:
                row_maximum(n + 2)
            if n + 3 + 1 < TILES_PER_BATCH:
                add_prior_and_mask(n + 3 + 1)

            if j == 0:
                if b >= 1:
                    transpose_e(8 * b - 2)
            elif j == 2:
                transpose_e(8 * b)
            elif j == 4:
                transpose_e(8 * b + 2)
            elif j == 6:
                transpose_e(8 * b + 4)
            if j == 0:
                if b + 1 < B:
                    waiting["q"] = transpose_heads(q_in[b + 1], 0)
            elif j == 1:
                if b + 1 < B:
                    waiting["x", 1] = transpose_x(b + 1, 2)
            elif j == 2:
                if b + 1 < B:
                    transpose_heads(q_in[b + 1], 1, waiting["q"])
            elif j == 3:
                if b + 1 < B:
                    transpose_x(b + 1, 3, waiting["x", 1])
            elif j == 4:
                if b + 2 < B:
                    waiting["k"] = transpose_heads(k_in[b + 2], 0)
            elif j == 5:
                if b + 2 < B:
                    waiting["x", 0] = transpose_x(b + 2, 0)
            elif j == 6:
                if b + 2 < B:
                    transpose_heads(k_in[b + 2], 1, waiting["k"])
            elif j == 7:
                if b + 2 < B:
                    transpose_x(b + 2, 1, waiting["x", 0])
            if n + 3 < TILES:
                multiply_queries_and_keys(n + 3)
            if j == 1:
                waiting["v", 0] = project_values(b, 0)
            elif j == 3:
                if b >= 1:
                    attend(2 * b - 1)
            elif j == 5:
                waiting["v", 1] = project_values(b, 1)
            elif j == 7:
                attend(2 * b)
            if n + 3 < TILES:
                add_bias_to_scores(n + 3)

            exponent(n)
            if j == 0:
                if 1 <= b < B - 1:
                    copy_x(b + 1, 0, waiting["x", 0])
            elif j == 1:
                if b >= 1:
                    group_e(8 * b - 2)
            elif j == 2:
                copy_values(b, 0, waiting["v", 0])
            elif j == 3:
                group_e(8 * b)
            elif j == 4:
                if b + 1 < B:
                    copy_x(b + 1, 1, waiting["x", 1])
            elif j == 5:
                group_e(8 * b + 2)
            elif j == 6:
                copy_values(b, 1, waiting["v", 1])
            elif j == 7 and b < B - 1:
                group_e(8 * b + 4)

        g = TILES // T - 1
        transpose_e(TILES - 2, 1, psum_s, "s")
        transpose_e(TILES - 1, 1, psum_s, "s")
        quantise_values(B - 1, 1)
        group_e(TILES - 4, 2, nc.vector.tensor_copy)
        divide_and_store(g - 1)
        quantise_e(g, 0, 2)
        group_e(TILES - 2, 1, nc.vector.tensor_copy)
        invert_row_sums(g)
        quantise_e(g, 2, 1)
        group_e(TILES - 1, 1)
        attend(g, 0, 3, psum_s, "s")
        quantise_e(g, 3, 1)
        attend(g, 3, 1, psum_s, "s")
        divide_and_store(g, 0, 3)
        divide_and_store(g, 3, 1, True)
